import numpy as np
import ml_dtypes

BF16 = ml_dtypes.bfloat16


def bf(x):
    return np.asarray(x, np.float32).astype(BF16)


def f32(x):
    return np.asarray(x, np.float32)


def f64(x):
    return np.asarray(x).astype(np.float64)


def striped(idx):
    return np.tile(idx.reshape(-1, 16).T, (8, 1))


D, S, H, N = 128, 4096, 128, 2048
SCALE = 1.0 / np.sqrt(D)


def setup_inputs():
    return {"qt": bf(np.random.standard_normal((D, H))), "k_pool": bf(np.random.standard_normal((D, S))), "v": bf(4.0 * np.random.standard_normal((N, D))), "sinks": f32(6.5 + 0.5 * np.random.standard_normal((H, 1))), "offs": striped(np.random.permutation(S)[:N])}


def reference(qt, k_pool, v, sinks, offs):
    idx = offs[:16].T.reshape(-1)
    s = SCALE * (f64(qt).T @ f64(k_pool)[:, idx])
    e = np.exp(s)
    den = np.exp(f64(sinks)) + e.sum(axis=1, keepdims=True)
    p = e / den
    return p @ f64(v)

@@ -1,0 +1,89 @@
+import math
+
+import concourse.mybir as mybir
+from concourse.masks import make_identity
+
+BF16, F32, U16 = mybir.dt.bfloat16, mybir.dt.float32, mybir.dt.uint16
+EXP = mybir.ActivationFunctionType.Exp
+MULT, MIN = mybir.AluOpType.mult, mybir.AluOpType.min
+ALONG_ROW = mybir.AxisListType.X
+
+D, S, H, N = 128, 4096, 128, 2048
+SCALE = 1.0 / math.sqrt(D)
+PIECE = 512
+N_PIECES = N // PIECE
+BLOCK = 128
+BLOCKS_PER_PIECE = PIECE // BLOCK
+N_BLOCKS = N // BLOCK
+
+FLOPS = 2 * H * D * N + 2 * H * N * D
+
+
+def tile_mm_kernel(tc, qt, k_pool, v, sinks, offs, out):
+    nc = tc.nc
+    with (
+        tc.tile_pool(name="held", bufs=1) as held,
+        tc.tile_pool(name="ring", bufs=2) as ring,
+        tc.psum_pool(name="score_banks", bufs=1) as score_banks,
+        tc.psum_pool(name="flip_banks", bufs=2) as flip_banks,
+        tc.psum_pool(name="out_bank", bufs=1) as out_bank,
+    ):
+        offsets = held.tile([128, N // 16], U16, name="offsets")
+        nc.sync.dma_start(offsets[:], offs)
+        keys = held.tile([D, S], BF16, name="keys")
+        nc.sync.dma_start(keys[:], k_pool)
+        queries = held.tile([D, H], BF16, name="queries")
+        nc.scalar.dma_start(queries[:], qt)
+        sink = held.tile([H, 1], F32, name="sink")
+        nc.scalar.dma_start(sink[:], sinks)
+        values = held.tile([BLOCK, N_BLOCKS, D], BF16, name="values")
+        nc.sync.dma_start(values[:], v.rearrange("(t p) e -> p t e", p=BLOCK))
+
+        identity = held.tile([H, H], BF16, name="identity")
+        make_identity(nc, identity[:])
+        neg_sink = held.tile([H, 1], F32, name="neg_sink")
+        nc.vector.tensor_scalar_mul(neg_sink[:], sink[:], -1.0)
+
+        scores = [score_banks.tile([H, PIECE], F32, name=f"scores{g}") for g in range(N_PIECES)]
+        piece_max = held.tile([H, N_PIECES], F32, name="piece_max")
+        for g in range(N_PIECES):
+            piece_offsets = offsets[:, g * (PIECE // 16) : (g + 1) * (PIECE // 16)]
+            nc.tensor.matmul(scores[g][:], queries[:], keys[:].indirect(piece_offsets), start=True, stop=True)
+            nc.vector.reduce_max(piece_max[:, g : g + 1], scores[g][:], axis=ALONG_ROW)
+
+        score_max = held.tile([H, 1], F32, name="score_max")
+        nc.vector.reduce_max(score_max[:], piece_max[:], axis=ALONG_ROW)
+        neg_shift = held.tile([H, 1], F32, name="neg_shift")
+        nc.vector.tensor_scalar(neg_shift[:], score_max[:], -SCALE, neg_sink[:, 0:1], op0=MULT, op1=MIN)
+
+        masses = held.tile([H, N_PIECES + 1], F32, name="masses")
+        mixed = out_bank.tile([H, D], F32, name="mixed")
+        for g in range(N_PIECES):
+            weights = ring.tile([H, PIECE], BF16, name="weights")
+            nc.scalar.activation(
+                weights[:], scores[g][:], EXP, bias=neg_shift[:, 0:1], scale=SCALE, accum_out=masses[:, g : g + 1]
+            )
+            flipped_bank = flip_banks.tile([BLOCK, PIECE], BF16, name="flipped_bank")
+            for b in range(BLOCKS_PER_PIECE):
+                block = slice(b * BLOCK, (b + 1) * BLOCK)
+                nc.tensor.transpose(flipped_bank[:, block], weights[:, block], identity[:])
+            flipped = ring.tile([BLOCK, PIECE], BF16, name="flipped")
+            nc.vector.tensor_copy(flipped[:], flipped_bank[:])
+            for b in range(BLOCKS_PER_PIECE):
+                t = g * BLOCKS_PER_PIECE + b
+                nc.tensor.matmul(
+                    mixed[:],
+                    flipped[:, b * BLOCK : (b + 1) * BLOCK],
+                    values[:, t, :],
+                    start=(t == 0),
+                    stop=(t == N_BLOCKS - 1),
+                )
+        nc.scalar.activation(masses[:, N_PIECES : N_PIECES + 1], sink[:], EXP, bias=neg_shift[:, 0:1], scale=1.0)
+
+        den = held.tile([H, 1], F32, name="den")
+        nc.vector.reduce_sum(den[:], masses[:], axis=ALONG_ROW)
+        inv_den = held.tile([H, 1], F32, name="inv_den")
+        nc.vector.reciprocal(inv_den[:], den[:])
+        result = held.tile([H, D], F32, name="result")
+        nc.vector.tensor_scalar_mul(result[:], mixed[:], inv_den[:, 0:1])
+        nc.sync.dma_start(out, result[:])

@@ -16,6 +16,8 @@ BLOCK = 128
 BLOCKS_PER_PIECE = PIECE // BLOCK
 N_BLOCKS = N // BLOCK
 
+WARM_UP_MATMULS = 8
+
 FLOPS = 2 * H * D * N + 2 * H * N * D
 
 
@@ -27,7 +29,14 @@ def tile_mm_kernel(tc, qt, k_pool, v, sinks, offs, out):
         tc.psum_pool(name="score_banks", bufs=1) as score_banks,
         tc.psum_pool(name="flip_banks", bufs=2) as flip_banks,
         tc.psum_pool(name="out_bank", bufs=1) as out_bank,
+        tc.psum_pool(name="idle_bank", bufs=1) as idle_bank,
     ):
+        zeros = held.tile([128, PIECE], BF16, name="zeros")
+        nc.gpsimd.memset(zeros[:], 0.0)
+        unused = idle_bank.tile([128, PIECE], F32, name="unused")
+        for i in range(WARM_UP_MATMULS):
+            nc.tensor.matmul(unused[:], zeros[:, 0:128], zeros[:], start=True, stop=True)
+
         offsets = held.tile([128, N // 16], U16, name="offsets")
         nc.sync.dma_start(offsets[:], offs)
         keys = held.tile([D, S], BF16, name="keys")

@@ -5,7 +5,7 @@ from concourse.masks import make_identity
 
 BF16, F32, U16 = mybir.dt.bfloat16, mybir.dt.float32, mybir.dt.uint16
 EXP = mybir.ActivationFunctionType.Exp
-MULT, MIN = mybir.AluOpType.mult, mybir.AluOpType.min
+MULT, ADD, MIN = mybir.AluOpType.mult, mybir.AluOpType.add, mybir.AluOpType.min
 ALONG_ROW = mybir.AxisListType.X
 
 D, S, H, N = 128, 4096, 128, 2048
@@ -15,8 +15,9 @@ N_PIECES = N // PIECE
 BLOCK = 128
 BLOCKS_PER_PIECE = PIECE // BLOCK
 N_BLOCKS = N // BLOCK
-
-WARM_UP_MATMULS = 8
+N_HALVES = 2
+PIECES_PER_HALF = N_PIECES // N_HALVES
+BLOCKS_PER_HALF = N_BLOCKS // N_HALVES
 
 FLOPS = 2 * H * D * N + 2 * H * N * D
 
@@ -28,15 +29,8 @@ def tile_mm_kernel(tc, qt, k_pool, v, sinks, offs, out):
         tc.tile_pool(name="ring", bufs=2) as ring,
         tc.psum_pool(name="score_banks", bufs=1) as score_banks,
         tc.psum_pool(name="flip_banks", bufs=2) as flip_banks,
-        tc.psum_pool(name="out_bank", bufs=1) as out_bank,
-        tc.psum_pool(name="idle_bank", bufs=1) as idle_bank,
+        tc.psum_pool(name="out_banks", bufs=1) as out_banks,
     ):
-        zeros = held.tile([128, PIECE], BF16, name="zeros")
-        nc.gpsimd.memset(zeros[:], 0.0)
-        unused = idle_bank.tile([128, PIECE], F32, name="unused")
-        for i in range(WARM_UP_MATMULS):
-            nc.tensor.matmul(unused[:], zeros[:, 0:128], zeros[:], start=True, stop=True)
-
         offsets = held.tile([128, N // 16], U16, name="offsets")
         nc.sync.dma_start(offsets[:], offs)
         keys = held.tile([D, S], BF16, name="keys")
@@ -50,27 +44,37 @@ def tile_mm_kernel(tc, qt, k_pool, v, sinks, offs, out):
 
         identity = held.tile([H, H], BF16, name="identity")
         make_identity(nc, identity[:])
-        neg_sink = held.tile([H, 1], F32, name="neg_sink")
-        nc.vector.tensor_scalar_mul(neg_sink[:], sink[:], -1.0)
+
+        neg_shift = held.tile([H, N_HALVES + 1], F32, name="neg_shift")
+        nc.vector.tensor_scalar_mul(neg_shift[:, 0:1], sink[:], -1.0)
 
         scores = [score_banks.tile([H, PIECE], F32, name=f"scores{g}") for g in range(N_PIECES)]
         piece_max = held.tile([H, N_PIECES], F32, name="piece_max")
-        for g in range(N_PIECES):
-            piece_offsets = offsets[:, g * (PIECE // 16) : (g + 1) * (PIECE // 16)]
-            nc.tensor.matmul(scores[g][:], queries[:], keys[:].indirect(piece_offsets), start=True, stop=True)
-            nc.vector.reduce_max(piece_max[:, g : g + 1], scores[g][:], axis=ALONG_ROW)
+        for k in range(N_HALVES):
+            for g in range(k * PIECES_PER_HALF, (k + 1) * PIECES_PER_HALF):
+                piece_offsets = offsets[:, g * (PIECE // 16) : (g + 1) * (PIECE // 16)]
+                nc.tensor.matmul(scores[g][:], queries[:], keys[:].indirect(piece_offsets), start=True, stop=True)
+                nc.vector.reduce_max(piece_max[:, g : g + 1], scores[g][:], axis=ALONG_ROW)
+            half_max = ring.tile([H, 1], F32, name="half_max")
+            nc.vector.reduce_max(
+                half_max[:], piece_max[:, k * PIECES_PER_HALF : (k + 1) * PIECES_PER_HALF], axis=ALONG_ROW
+            )
+            nc.vector.tensor_scalar(
+                neg_shift[:, k + 1 : k + 2], half_max[:], -SCALE, neg_shift[:, k : k + 1], op0=MULT, op1=MIN
+            )
 
-        score_max = held.tile([H, 1], F32, name="score_max")
-        nc.vector.reduce_max(score_max[:], piece_max[:], axis=ALONG_ROW)
-        neg_shift = held.tile([H, 1], F32, name="neg_shift")
-        nc.vector.tensor_scalar(neg_shift[:], score_max[:], -SCALE, neg_sink[:, 0:1], op0=MULT, op1=MIN)
-
-        masses = held.tile([H, N_PIECES + 1], F32, name="masses")
-        mixed = out_bank.tile([H, D], F32, name="mixed")
+        masses = held.tile([H, N_PIECES], F32, name="masses")
+        partial = [out_banks.tile([H, D], F32, name=f"partial{k}") for k in range(N_HALVES)]
         for g in range(N_PIECES):
+            k = g // PIECES_PER_HALF
             weights = ring.tile([H, PIECE], BF16, name="weights")
             nc.scalar.activation(
-                weights[:], scores[g][:], EXP, bias=neg_shift[:, 0:1], scale=SCALE, accum_out=masses[:, g : g + 1]
+                weights[:],
+                scores[g][:],
+                EXP,
+                bias=neg_shift[:, k + 1 : k + 2],
+                scale=SCALE,
+                accum_out=masses[:, g : g + 1],
             )
             flipped_bank = flip_banks.tile([BLOCK, PIECE], BF16, name="flipped_bank")
             for b in range(BLOCKS_PER_PIECE):
@@ -81,18 +85,31 @@ def tile_mm_kernel(tc, qt, k_pool, v, sinks, offs, out):
             for b in range(BLOCKS_PER_PIECE):
                 t = g * BLOCKS_PER_PIECE + b
                 nc.tensor.matmul(
-                    mixed[:],
+                    partial[k][:],
                     flipped[:, b * BLOCK : (b + 1) * BLOCK],
                     values[:, t, :],
-                    start=(t == 0),
-                    stop=(t == N_BLOCKS - 1),
+                    start=(t % BLOCKS_PER_HALF == 0),
+                    stop=(t % BLOCKS_PER_HALF == BLOCKS_PER_HALF - 1),
                 )
-        nc.scalar.activation(masses[:, N_PIECES : N_PIECES + 1], sink[:], EXP, bias=neg_shift[:, 0:1], scale=1.0)
 
+        rescale = held.tile([H, N_HALVES], F32, name="rescale")
+        nc.scalar.activation(
+            rescale[:], neg_shift[:, 0:N_HALVES], EXP, bias=neg_shift[:, N_HALVES : N_HALVES + 1], scale=-1.0
+        )
+        half_mass = held.tile([H, N_HALVES], F32, name="half_mass")
+        nc.vector.reduce_sum(half_mass[:], masses[:].rearrange("h (k p) -> h k p", p=PIECES_PER_HALF), axis=ALONG_ROW)
+        early_den = held.tile([H, 1], F32, name="early_den")
+        nc.vector.tensor_scalar(
+            early_den[:], half_mass[:, 0:1], rescale[:, 1:2], rescale[:, 0:1], op0=MULT, op1=ADD
+        )
         den = held.tile([H, 1], F32, name="den")
-        nc.vector.reduce_sum(den[:], masses[:], axis=ALONG_ROW)
+        nc.vector.tensor_add(den[:], early_den[:], half_mass[:, 1:2])
         inv_den = held.tile([H, 1], F32, name="inv_den")
         nc.vector.reciprocal(inv_den[:], den[:])
+        early_factor = held.tile([H, 1], F32, name="early_factor")
+        nc.vector.tensor_mul(early_factor[:], rescale[:, 1:2], inv_den[:])
+        early = held.tile([H, D], F32, name="early")
+        nc.vector.tensor_scalar_mul(early[:], partial[0][:], early_factor[:, 0:1])
         result = held.tile([H, D], F32, name="result")
-        nc.vector.tensor_scalar_mul(result[:], mixed[:], inv_den[:, 0:1])
+        nc.vector.scalar_tensor_tensor(result[:], partial[1][:], inv_den[:, 0:1], early[:], op0=MULT, op1=ADD)
         nc.sync.dma_start(out, result[:])

@@ -5,7 +5,7 @@ from concourse.masks import make_identity
 
 BF16, F32, U16 = mybir.dt.bfloat16, mybir.dt.float32, mybir.dt.uint16
 EXP = mybir.ActivationFunctionType.Exp
-MULT, ADD, MIN = mybir.AluOpType.mult, mybir.AluOpType.add, mybir.AluOpType.min
+MULT, MIN = mybir.AluOpType.mult, mybir.AluOpType.min
 ALONG_ROW = mybir.AxisListType.X
 
 D, S, H, N = 128, 4096, 128, 2048
@@ -15,9 +15,6 @@ N_PIECES = N // PIECE
 BLOCK = 128
 BLOCKS_PER_PIECE = PIECE // BLOCK
 N_BLOCKS = N // BLOCK
-N_HALVES = 2
-PIECES_PER_HALF = N_PIECES // N_HALVES
-BLOCKS_PER_HALF = N_BLOCKS // N_HALVES
 
 FLOPS = 2 * H * D * N + 2 * H * N * D
 
@@ -29,7 +26,7 @@ def tile_mm_kernel(tc, qt, k_pool, v, sinks, offs, out):
         tc.tile_pool(name="ring", bufs=2) as ring,
         tc.psum_pool(name="score_banks", bufs=1) as score_banks,
         tc.psum_pool(name="flip_banks", bufs=2) as flip_banks,
-        tc.psum_pool(name="out_banks", bufs=1) as out_banks,
+        tc.psum_pool(name="out_bank", bufs=1) as out_bank,
     ):
         offsets = held.tile([128, N // 16], U16, name="offsets")
         nc.sync.dma_start(offsets[:], offs)
@@ -39,77 +36,57 @@ def tile_mm_kernel(tc, qt, k_pool, v, sinks, offs, out):
         nc.scalar.dma_start(queries[:], qt)
         sink = held.tile([H, 1], F32, name="sink")
         nc.scalar.dma_start(sink[:], sinks)
-        values = held.tile([BLOCK, N_BLOCKS, D], BF16, name="values")
-        nc.sync.dma_start(values[:], v.rearrange("(t p) e -> p t e", p=BLOCK))
+        values = held.tile([BLOCK, N_PIECES, BLOCKS_PER_PIECE, D], BF16, name="values")
+        nc.sync.dma_start(
+            values[:].rearrange("p g b e -> p g (b e)"),
+            v.rearrange("(g p b) e -> p g (b e)", g=N_PIECES, b=BLOCKS_PER_PIECE),
+        )
 
         identity = held.tile([H, H], BF16, name="identity")
         make_identity(nc, identity[:])
-
-        neg_shift = held.tile([H, N_HALVES + 1], F32, name="neg_shift")
-        nc.vector.tensor_scalar_mul(neg_shift[:, 0:1], sink[:], -1.0)
+        neg_sink = held.tile([H, 1], F32, name="neg_sink")
+        nc.vector.tensor_scalar_mul(neg_sink[:], sink[:], -1.0)
 
         scores = [score_banks.tile([H, PIECE], F32, name=f"scores{g}") for g in range(N_PIECES)]
         piece_max = held.tile([H, N_PIECES], F32, name="piece_max")
-        for k in range(N_HALVES):
-            for g in range(k * PIECES_PER_HALF, (k + 1) * PIECES_PER_HALF):
-                piece_offsets = offsets[:, g * (PIECE // 16) : (g + 1) * (PIECE // 16)]
-                nc.tensor.matmul(scores[g][:], queries[:], keys[:].indirect(piece_offsets), start=True, stop=True)
-                nc.vector.reduce_max(piece_max[:, g : g + 1], scores[g][:], axis=ALONG_ROW)
-            half_max = ring.tile([H, 1], F32, name="half_max")
-            nc.vector.reduce_max(
-                half_max[:], piece_max[:, k * PIECES_PER_HALF : (k + 1) * PIECES_PER_HALF], axis=ALONG_ROW
-            )
-            nc.vector.tensor_scalar(
-                neg_shift[:, k + 1 : k + 2], half_max[:], -SCALE, neg_shift[:, k : k + 1], op0=MULT, op1=MIN
-            )
-
-        masses = held.tile([H, N_PIECES], F32, name="masses")
-        partial = [out_banks.tile([H, D], F32, name=f"partial{k}") for k in range(N_HALVES)]
         for g in range(N_PIECES):
-            k = g // PIECES_PER_HALF
+            piece_offsets = offsets[:, g * (PIECE // 16) : (g + 1) * (PIECE // 16)]
+            nc.tensor.matmul(scores[g][:], queries[:], keys[:].indirect(piece_offsets), start=True, stop=True)
+            nc.vector.reduce_max(piece_max[:, g : g + 1], scores[g][:], axis=ALONG_ROW)
+
+        score_max = held.tile([H, 1], F32, name="score_max")
+        nc.vector.reduce_max(score_max[:], piece_max[:], axis=ALONG_ROW)
+        neg_shift = held.tile([H, 1], F32, name="neg_shift")
+        nc.vector.tensor_scalar(neg_shift[:], score_max[:], -SCALE, neg_sink[:, 0:1], op0=MULT, op1=MIN)
+
+        masses = held.tile([H, N_PIECES + 1], F32, name="masses")
+        mixed = out_bank.tile([H, D], F32, name="mixed")
+        for g in range(N_PIECES):
             weights = ring.tile([H, PIECE], BF16, name="weights")
             nc.scalar.activation(
-                weights[:],
-                scores[g][:],
-                EXP,
-                bias=neg_shift[:, k + 1 : k + 2],
-                scale=SCALE,
-                accum_out=masses[:, g : g + 1],
+                weights[:], scores[g][:], EXP, bias=neg_shift[:, 0:1], scale=SCALE, accum_out=masses[:, g : g + 1]
             )
             flipped_bank = flip_banks.tile([BLOCK, PIECE], BF16, name="flipped_bank")
+            weights_by_block = weights[:].rearrange("h (p b) -> h b p", b=BLOCKS_PER_PIECE)
             for b in range(BLOCKS_PER_PIECE):
-                block = slice(b * BLOCK, (b + 1) * BLOCK)
-                nc.tensor.transpose(flipped_bank[:, block], weights[:, block], identity[:])
+                nc.tensor.transpose(flipped_bank[:, b * BLOCK : (b + 1) * BLOCK], weights_by_block[:, b, :], identity[:])
             flipped = ring.tile([BLOCK, PIECE], BF16, name="flipped")
             nc.vector.tensor_copy(flipped[:], flipped_bank[:])
             for b in range(BLOCKS_PER_PIECE):
                 t = g * BLOCKS_PER_PIECE + b
                 nc.tensor.matmul(
-                    partial[k][:],
+                    mixed[:],
                     flipped[:, b * BLOCK : (b + 1) * BLOCK],
-                    values[:, t, :],
-                    start=(t % BLOCKS_PER_HALF == 0),
-                    stop=(t % BLOCKS_PER_HALF == BLOCKS_PER_HALF - 1),
+                    values[:, g, b, :],
+                    start=(t == 0),
+                    stop=(t == N_BLOCKS - 1),
                 )
+        nc.scalar.activation(masses[:, N_PIECES : N_PIECES + 1], sink[:], EXP, bias=neg_shift[:, 0:1], scale=1.0)
 
-        rescale = held.tile([H, N_HALVES], F32, name="rescale")
-        nc.scalar.activation(
-            rescale[:], neg_shift[:, 0:N_HALVES], EXP, bias=neg_shift[:, N_HALVES : N_HALVES + 1], scale=-1.0
-        )
-        half_mass = held.tile([H, N_HALVES], F32, name="half_mass")
-        nc.vector.reduce_sum(half_mass[:], masses[:].rearrange("h (k p) -> h k p", p=PIECES_PER_HALF), axis=ALONG_ROW)
-        early_den = held.tile([H, 1], F32, name="early_den")
-        nc.vector.tensor_scalar(
-            early_den[:], half_mass[:, 0:1], rescale[:, 1:2], rescale[:, 0:1], op0=MULT, op1=ADD
-        )
         den = held.tile([H, 1], F32, name="den")
-        nc.vector.tensor_add(den[:], early_den[:], half_mass[:, 1:2])
+        nc.vector.reduce_sum(den[:], masses[:], axis=ALONG_ROW)
         inv_den = held.tile([H, 1], F32, name="inv_den")
         nc.vector.reciprocal(inv_den[:], den[:])
-        early_factor = held.tile([H, 1], F32, name="early_factor")
-        nc.vector.tensor_mul(early_factor[:], rescale[:, 1:2], inv_den[:])
-        early = held.tile([H, D], F32, name="early")
-        nc.vector.tensor_scalar_mul(early[:], partial[0][:], early_factor[:, 0:1])
         result = held.tile([H, D], F32, name="result")
-        nc.vector.scalar_tensor_tensor(result[:], partial[1][:], inv_den[:, 0:1], early[:], op0=MULT, op1=ADD)
+        nc.vector.tensor_scalar_mul(result[:], mixed[:], inv_den[:, 0:1])
         nc.sync.dma_start(out, result[:])

@@ -5,7 +5,7 @@ from concourse.masks import make_identity
 
 BF16, F32, U16 = mybir.dt.bfloat16, mybir.dt.float32, mybir.dt.uint16
 EXP = mybir.ActivationFunctionType.Exp
-MULT, MIN = mybir.AluOpType.mult, mybir.AluOpType.min
+MULT, ADD, MIN = mybir.AluOpType.mult, mybir.AluOpType.add, mybir.AluOpType.min
 ALONG_ROW = mybir.AxisListType.X
 
 D, S, H, N = 128, 4096, 128, 2048
@@ -15,6 +15,7 @@ N_PIECES = N // PIECE
 BLOCK = 128
 BLOCKS_PER_PIECE = PIECE // BLOCK
 N_BLOCKS = N // BLOCK
+N_BEFORE_DEN = N_PIECES // 2
 
 FLOPS = 2 * H * D * N + 2 * H * N * D
 
@@ -26,7 +27,7 @@ def tile_mm_kernel(tc, qt, k_pool, v, sinks, offs, out):
         tc.tile_pool(name="ring", bufs=2) as ring,
         tc.psum_pool(name="score_banks", bufs=1) as score_banks,
         tc.psum_pool(name="flip_banks", bufs=2) as flip_banks,
-        tc.psum_pool(name="out_bank", bufs=1) as out_bank,
+        tc.psum_pool(name="out_banks", bufs=1) as out_banks,
     ):
         offsets = held.tile([128, N // 16], U16, name="offsets")
         nc.sync.dma_start(offsets[:], offs)
@@ -44,27 +45,35 @@ def tile_mm_kernel(tc, qt, k_pool, v, sinks, offs, out):
 
         identity = held.tile([H, H], BF16, name="identity")
         make_identity(nc, identity[:])
-        neg_sink = held.tile([H, 1], F32, name="neg_sink")
-        nc.vector.tensor_scalar_mul(neg_sink[:], sink[:], -1.0)
+
+        neg_shift = held.tile([H, N_PIECES + 1], F32, name="neg_shift")
+        nc.vector.tensor_scalar_mul(neg_shift[:, 0:1], sink[:], -1.0)
 
         scores = [score_banks.tile([H, PIECE], F32, name=f"scores{g}") for g in range(N_PIECES)]
-        piece_max = held.tile([H, N_PIECES], F32, name="piece_max")
         for g in range(N_PIECES):
             piece_offsets = offsets[:, g * (PIECE // 16) : (g + 1) * (PIECE // 16)]
             nc.tensor.matmul(scores[g][:], queries[:], keys[:].indirect(piece_offsets), start=True, stop=True)
-            nc.vector.reduce_max(piece_max[:, g : g + 1], scores[g][:], axis=ALONG_ROW)
+            neg_logits = ring.tile([H, PIECE], F32, name="neg_logits")
+            nc.vector.tensor_scalar(
+                neg_logits[:], scores[g][:], -SCALE, None, op0=MULT, op1=MIN, accum_out=neg_shift[:, g + 1 : g + 2]
+            )
+        neg_common = held.tile([H, 1], F32, name="neg_common")
+        nc.vector.tensor_reduce(neg_common[:], neg_shift[:], axis=ALONG_ROW, op=MIN)
 
-        score_max = held.tile([H, 1], F32, name="score_max")
-        nc.vector.reduce_max(score_max[:], piece_max[:], axis=ALONG_ROW)
-        neg_shift = held.tile([H, 1], F32, name="neg_shift")
-        nc.vector.tensor_scalar(neg_shift[:], score_max[:], -SCALE, neg_sink[:, 0:1], op0=MULT, op1=MIN)
-
-        masses = held.tile([H, N_PIECES + 1], F32, name="masses")
-        mixed = out_bank.tile([H, D], F32, name="mixed")
+        mass = held.tile([H, N_PIECES + 1], F32, name="mass")
+        nc.vector.memset(mass[:], 1.0)
+        early_bank = out_banks.tile([H, N_PIECES - 1, D], F32, name="early_bank")
+        last_bank = out_banks.tile([H, D], F32, name="last_bank")
+        partial = [early_bank[:, g, :] for g in range(N_PIECES - 1)] + [last_bank[:]]
         for g in range(N_PIECES):
             weights = ring.tile([H, PIECE], BF16, name="weights")
             nc.scalar.activation(
-                weights[:], scores[g][:], EXP, bias=neg_shift[:, 0:1], scale=SCALE, accum_out=masses[:, g : g + 1]
+                weights[:],
+                scores[g][:],
+                EXP,
+                bias=neg_shift[:, g + 1 : g + 2],
+                scale=SCALE,
+                accum_out=mass[:, g + 1 : g + 2],
             )
             flipped_bank = flip_banks.tile([BLOCK, PIECE], BF16, name="flipped_bank")
             weights_by_block = weights[:].rearrange("h (p b) -> h b p", b=BLOCKS_PER_PIECE)
@@ -73,20 +82,36 @@ def tile_mm_kernel(tc, qt, k_pool, v, sinks, offs, out):
             flipped = ring.tile([BLOCK, PIECE], BF16, name="flipped")
             nc.vector.tensor_copy(flipped[:], flipped_bank[:])
             for b in range(BLOCKS_PER_PIECE):
-                t = g * BLOCKS_PER_PIECE + b
                 nc.tensor.matmul(
-                    mixed[:],
+                    partial[g],
                     flipped[:, b * BLOCK : (b + 1) * BLOCK],
                     values[:, g, b, :],
-                    start=(t == 0),
-                    stop=(t == N_BLOCKS - 1),
+                    start=(b == 0),
+                    stop=(b == BLOCKS_PER_PIECE - 1),
                 )
-        nc.scalar.activation(masses[:, N_PIECES : N_PIECES + 1], sink[:], EXP, bias=neg_shift[:, 0:1], scale=1.0)
 
+        rescale = held.tile([H, N_PIECES + 1], F32, name="rescale")
+        nc.scalar.activation(rescale[:], neg_shift[:], EXP, bias=neg_common[:, 0:1], scale=-1.0)
+
+        merged = held.tile([H, D], F32, name="merged0")
+        nc.vector.tensor_scalar_mul(merged[:], partial[0], rescale[:, 1:2])
+        for g in range(1, N_BEFORE_DEN):
+            longer = held.tile([H, D], F32, name=f"merged{g}")
+            nc.vector.scalar_tensor_tensor(longer[:], partial[g], rescale[:, g + 1 : g + 2], merged[:], op0=MULT, op1=ADD)
+            merged = longer
+
+        terms = held.tile([H, N_PIECES + 1], F32, name="terms")
         den = held.tile([H, 1], F32, name="den")
-        nc.vector.reduce_sum(den[:], masses[:], axis=ALONG_ROW)
+        nc.vector.scalar_tensor_tensor(terms[:], mass[:], 1.0, rescale[:], op0=MULT, op1=MULT, accum_out=den[:])
         inv_den = held.tile([H, 1], F32, name="inv_den")
         nc.vector.reciprocal(inv_den[:], den[:])
-        result = held.tile([H, D], F32, name="result")
-        nc.vector.tensor_scalar_mul(result[:], mixed[:], inv_den[:, 0:1])
-        nc.sync.dma_start(out, result[:])
+        factor = held.tile([H, N_PIECES + 1], F32, name="factor")
+        nc.vector.tensor_scalar_mul(factor[:], rescale[:], inv_den[:, 0:1])
+        divided = held.tile([H, D], F32, name="divided")
+        nc.vector.tensor_scalar_mul(divided[:], merged[:], inv_den[:, 0:1])
+        merged = divided
+        for g in range(N_BEFORE_DEN, N_PIECES):
+            longer = held.tile([H, D], F32, name=f"merged{g}")
+            nc.vector.scalar_tensor_tensor(longer[:], partial[g], factor[:, g + 1 : g + 2], merged[:], op0=MULT, op1=ADD)
+            merged = longer
+        nc.sync.dma_start(out, merged[:])

@@ -15,7 +15,6 @@ N_PIECES = N // PIECE
 BLOCK = 128
 BLOCKS_PER_PIECE = PIECE // BLOCK
 N_BLOCKS = N // BLOCK
-N_BEFORE_DEN = N_PIECES // 2
 
 FLOPS = 2 * H * D * N + 2 * H * N * D
 
@@ -62,43 +61,48 @@ def tile_mm_kernel(tc, qt, k_pool, v, sinks, offs, out):
 
         mass = held.tile([H, N_PIECES + 1], F32, name="mass")
         nc.vector.memset(mass[:], 1.0)
+        rescale = held.tile([H, N_PIECES + 1], F32, name="rescale")
         early_bank = out_banks.tile([H, N_PIECES - 1, D], F32, name="early_bank")
         last_bank = out_banks.tile([H, D], F32, name="last_bank")
         partial = [early_bank[:, g, :] for g in range(N_PIECES - 1)] + [last_bank[:]]
-        for g in range(N_PIECES):
-            weights = ring.tile([H, PIECE], BF16, name="weights")
-            nc.scalar.activation(
-                weights[:],
-                scores[g][:],
-                EXP,
-                bias=neg_shift[:, g + 1 : g + 2],
-                scale=SCALE,
-                accum_out=mass[:, g + 1 : g + 2],
-            )
-            flipped_bank = flip_banks.tile([BLOCK, PIECE], BF16, name="flipped_bank")
-            weights_by_block = weights[:].rearrange("h (p b) -> h b p", b=BLOCKS_PER_PIECE)
-            for b in range(BLOCKS_PER_PIECE):
-                nc.tensor.transpose(flipped_bank[:, b * BLOCK : (b + 1) * BLOCK], weights_by_block[:, b, :], identity[:])
-            flipped = ring.tile([BLOCK, PIECE], BF16, name="flipped")
-            nc.vector.tensor_copy(flipped[:], flipped_bank[:])
-            for b in range(BLOCKS_PER_PIECE):
-                nc.tensor.matmul(
-                    partial[g],
-                    flipped[:, b * BLOCK : (b + 1) * BLOCK],
-                    values[:, g, b, :],
-                    start=(b == 0),
-                    stop=(b == BLOCKS_PER_PIECE - 1),
+
+        flipped_banks = []
+        for step in range(N_PIECES + 1):
+            if step < N_PIECES:
+                g = step
+                weights = ring.tile([H, PIECE], BF16, name="weights")
+                nc.scalar.activation(
+                    weights[:],
+                    scores[g][:],
+                    EXP,
+                    bias=neg_shift[:, g + 1 : g + 2],
+                    scale=SCALE,
+                    accum_out=mass[:, g + 1 : g + 2],
                 )
-
-        rescale = held.tile([H, N_PIECES + 1], F32, name="rescale")
-        nc.scalar.activation(rescale[:], neg_shift[:], EXP, bias=neg_common[:, 0:1], scale=-1.0)
-
-        merged = held.tile([H, D], F32, name="merged0")
-        nc.vector.tensor_scalar_mul(merged[:], partial[0], rescale[:, 1:2])
-        for g in range(1, N_BEFORE_DEN):
-            longer = held.tile([H, D], F32, name=f"merged{g}")
-            nc.vector.scalar_tensor_tensor(longer[:], partial[g], rescale[:, g + 1 : g + 2], merged[:], op0=MULT, op1=ADD)
-            merged = longer
+                flipped_bank = flip_banks.tile([BLOCK, PIECE], BF16, name="flipped_bank")
+                weights_by_block = weights[:].rearrange("h (p b) -> h b p", b=BLOCKS_PER_PIECE)
+                for b in range(BLOCKS_PER_PIECE):
+                    nc.tensor.transpose(
+                        flipped_bank[:, b * BLOCK : (b + 1) * BLOCK], weights_by_block[:, b, :], identity[:]
+                    )
+                flipped_banks.append(flipped_bank)
+                if g == N_PIECES - 1:
+                    nc.scalar.activation(rescale[:], neg_shift[:], EXP, bias=neg_common[:, 0:1], scale=-1.0)
+            if step > 0:
+                g = step - 1
+                flipped = ring.tile([BLOCK, PIECE], BF16, name="flipped")
+                if g < N_PIECES - 1:
+                    nc.vector.tensor_copy(flipped[:], flipped_banks[g][:])
+                else:
+                    nc.scalar.copy(flipped[:], flipped_banks[g][:])
+                for b in range(BLOCKS_PER_PIECE):
+                    nc.tensor.matmul(
+                        partial[g],
+                        flipped[:, b * BLOCK : (b + 1) * BLOCK],
+                        values[:, g, b, :],
+                        start=(b == 0),
+                        stop=(b == BLOCKS_PER_PIECE - 1),
+                    )
 
         terms = held.tile([H, N_PIECES + 1], F32, name="terms")
         den = held.tile([H, 1], F32, name="den")
@@ -107,10 +111,9 @@ def tile_mm_kernel(tc, qt, k_pool, v, sinks, offs, out):
         nc.vector.reciprocal(inv_den[:], den[:])
         factor = held.tile([H, N_PIECES + 1], F32, name="factor")
         nc.vector.tensor_scalar_mul(factor[:], rescale[:], inv_den[:, 0:1])
-        divided = held.tile([H, D], F32, name="divided")
-        nc.vector.tensor_scalar_mul(divided[:], merged[:], inv_den[:, 0:1])
-        merged = divided
-        for g in range(N_BEFORE_DEN, N_PIECES):
+        merged = held.tile([H, D], F32, name="merged0")
+        nc.vector.tensor_scalar_mul(merged[:], partial[0], factor[:, 1:2])
+        for g in range(1, N_PIECES):
             longer = held.tile([H, D], F32, name=f"merged{g}")
             nc.vector.scalar_tensor_tensor(longer[:], partial[g], factor[:, g + 1 : g + 2], merged[:], op0=MULT, op1=ADD)
             merged = longer

@@ -12,21 +12,27 @@ D, S, H, N = 128, 4096, 128, 2048
 SCALE = 1.0 / math.sqrt(D)
 PIECE = 512
 N_PIECES = N // PIECE
+LAST = N_PIECES - 1
 BLOCK = 128
-BLOCKS_PER_PIECE = PIECE // BLOCK
-N_BLOCKS = N // BLOCK
+LAST_PIECE_CHUNKS = (256, 128, 128)
 
 FLOPS = 2 * H * D * N + 2 * H * N * D
 
 
 def tile_mm_kernel(tc, qt, k_pool, v, sinks, offs, out):
     nc = tc.nc
+    chunks = []
+    for g in range(N_PIECES):
+        first = 0
+        for width in LAST_PIECE_CHUNKS if g == LAST else (PIECE,):
+            chunks.append((g, first, width))
+            first += width
+    n_chunks = len(chunks)
+
     with (
         tc.tile_pool(name="held", bufs=1) as held,
         tc.tile_pool(name="ring", bufs=2) as ring,
-        tc.psum_pool(name="score_banks", bufs=1) as score_banks,
-        tc.psum_pool(name="flip_banks", bufs=2) as flip_banks,
-        tc.psum_pool(name="out_banks", bufs=1) as out_banks,
+        tc.psum_pool(name="banks", bufs=8) as banks,
     ):
         offsets = held.tile([128, N // 16], U16, name="offsets")
         nc.sync.dma_start(offsets[:], offs)
@@ -36,11 +42,15 @@ def tile_mm_kernel(tc, qt, k_pool, v, sinks, offs, out):
         nc.scalar.dma_start(queries[:], qt)
         sink = held.tile([H, 1], F32, name="sink")
         nc.scalar.dma_start(sink[:], sinks)
-        values = held.tile([BLOCK, N_PIECES, BLOCKS_PER_PIECE, D], BF16, name="values")
-        nc.sync.dma_start(
-            values[:].rearrange("p g b e -> p g (b e)"),
-            v.rearrange("(g p b) e -> p g (b e)", g=N_PIECES, b=BLOCKS_PER_PIECE),
-        )
+        values = []
+        for c, (g, first, width) in enumerate(chunks):
+            blocks = width // BLOCK
+            chunk_values = held.tile([BLOCK, blocks, D], BF16, name=f"values{c}")
+            chunk_rows = v[g * PIECE + first : g * PIECE + first + width, :]
+            nc.sync.dma_start(
+                chunk_values[:].rearrange("p b e -> p (b e)"), chunk_rows.rearrange("(p b) e -> p (b e)", b=blocks)
+            )
+            values.append(chunk_values)
 
         identity = held.tile([H, H], BF16, name="identity")
         make_identity(nc, identity[:])
@@ -48,7 +58,7 @@ def tile_mm_kernel(tc, qt, k_pool, v, sinks, offs, out):
         neg_shift = held.tile([H, N_PIECES + 1], F32, name="neg_shift")
         nc.vector.tensor_scalar_mul(neg_shift[:, 0:1], sink[:], -1.0)
 
-        scores = [score_banks.tile([H, PIECE], F32, name=f"scores{g}") for g in range(N_PIECES)]
+        scores = [banks.tile([H, PIECE], F32, name=f"scores{g}", tag="bank") for g in range(N_PIECES)]
         for g in range(N_PIECES):
             piece_offsets = offsets[:, g * (PIECE // 16) : (g + 1) * (PIECE // 16)]
             nc.tensor.matmul(scores[g][:], queries[:], keys[:].indirect(piece_offsets), start=True, stop=True)
@@ -59,62 +69,86 @@ def tile_mm_kernel(tc, qt, k_pool, v, sinks, offs, out):
         neg_common = held.tile([H, 1], F32, name="neg_common")
         nc.vector.tensor_reduce(neg_common[:], neg_shift[:], axis=ALONG_ROW, op=MIN)
 
-        mass = held.tile([H, N_PIECES + 1], F32, name="mass")
+        mass = held.tile([H, n_chunks + 1], F32, name="mass")
         nc.vector.memset(mass[:], 1.0)
         rescale = held.tile([H, N_PIECES + 1], F32, name="rescale")
-        early_bank = out_banks.tile([H, N_PIECES - 1, D], F32, name="early_bank")
-        last_bank = out_banks.tile([H, D], F32, name="last_bank")
-        partial = [early_bank[:, g, :] for g in range(N_PIECES - 1)] + [last_bank[:]]
 
         flipped_banks = []
-        for step in range(N_PIECES + 1):
-            if step < N_PIECES:
-                g = step
-                weights = ring.tile([H, PIECE], BF16, name="weights")
+        partial = []
+        for step in range(n_chunks + 1):
+            if step < n_chunks:
+                g, first, width = chunks[step]
+                blocks = width // BLOCK
+                weights = held.tile([H, width], BF16, name=f"weights{step}")
                 nc.scalar.activation(
                     weights[:],
-                    scores[g][:],
+                    scores[g][:, first : first + width],
                     EXP,
                     bias=neg_shift[:, g + 1 : g + 2],
                     scale=SCALE,
-                    accum_out=mass[:, g + 1 : g + 2],
+                    accum_out=mass[:, step + 1 : step + 2],
                 )
-                flipped_bank = flip_banks.tile([BLOCK, PIECE], BF16, name="flipped_bank")
-                weights_by_block = weights[:].rearrange("h (p b) -> h b p", b=BLOCKS_PER_PIECE)
-                for b in range(BLOCKS_PER_PIECE):
+                flipped_bank = banks.tile([BLOCK, width], BF16, name=f"flipped_bank{step}", tag="bank")
+                weights_by_block = weights[:].rearrange("h (p b) -> h b p", b=blocks)
+                for b in range(blocks):
                     nc.tensor.transpose(
                         flipped_bank[:, b * BLOCK : (b + 1) * BLOCK], weights_by_block[:, b, :], identity[:]
                     )
                 flipped_banks.append(flipped_bank)
-                if g == N_PIECES - 1:
+                if g == LAST and first == 0:
                     nc.scalar.activation(rescale[:], neg_shift[:], EXP, bias=neg_common[:, 0:1], scale=-1.0)
             if step > 0:
-                g = step - 1
-                flipped = ring.tile([BLOCK, PIECE], BF16, name="flipped")
-                if g < N_PIECES - 1:
-                    nc.vector.tensor_copy(flipped[:], flipped_banks[g][:])
+                c = step - 1
+                g, first, width = chunks[c]
+                blocks = width // BLOCK
+                flipped = held.tile([BLOCK, width], BF16, name=f"flipped{c}")
+                if g == LAST and first > 0:
+                    nc.scalar.copy(flipped[:], flipped_banks[c][:])
                 else:
-                    nc.scalar.copy(flipped[:], flipped_banks[g][:])
-                for b in range(BLOCKS_PER_PIECE):
+                    nc.vector.tensor_copy(flipped[:], flipped_banks[c][:])
+                if first == 0:
+                    partial.append(banks.tile([H, D], F32, name=f"partial{g}", tag="bank"))
+                for b in range(blocks):
                     nc.tensor.matmul(
-                        partial[g],
+                        partial[g][:],
                         flipped[:, b * BLOCK : (b + 1) * BLOCK],
-                        values[:, g, b, :],
-                        start=(b == 0),
-                        stop=(b == BLOCKS_PER_PIECE - 1),
+                        values[c][:, b, :],
+                        start=(first == 0 and b == 0),
+                        stop=(first + width == PIECE and b == blocks - 1),
                     )
 
-        terms = held.tile([H, N_PIECES + 1], F32, name="terms")
+        merged0 = held.tile([H, D], F32, name="merged0")
+        nc.vector.tensor_scalar_mul(merged0[:], partial[0][:], rescale[:, 1:2])
+        merged1 = held.tile([H, D], F32, name="merged1")
+        nc.vector.scalar_tensor_tensor(merged1[:], partial[1][:], rescale[:, 2:3], merged0[:], op0=MULT, op1=ADD)
+        early_terms = held.tile([H, N_PIECES], F32, name="early_terms")
+        early_den = held.tile([H, 1], F32, name="early_den")
+        nc.vector.scalar_tensor_tensor(
+            early_terms[:], mass[:, 0:N_PIECES], 1.0, rescale[:, 0:N_PIECES], op0=MULT, op1=MULT, accum_out=early_den[:]
+        )
+        last_terms = held.tile([H, n_chunks - LAST], F32, name="last_terms")
         den = held.tile([H, 1], F32, name="den")
-        nc.vector.scalar_tensor_tensor(terms[:], mass[:], 1.0, rescale[:], op0=MULT, op1=MULT, accum_out=den[:])
+        nc.vector.tensor_scalar(
+            last_terms[:],
+            mass[:, N_PIECES : n_chunks + 1],
+            rescale[:, N_PIECES : N_PIECES + 1],
+            early_den[:, 0:1],
+            op0=MULT,
+            op1=ADD,
+            accum_out=den[:],
+        )
         inv_den = held.tile([H, 1], F32, name="inv_den")
         nc.vector.reciprocal(inv_den[:], den[:])
-        factor = held.tile([H, N_PIECES + 1], F32, name="factor")
-        nc.vector.tensor_scalar_mul(factor[:], rescale[:], inv_den[:, 0:1])
-        merged = held.tile([H, D], F32, name="merged0")
-        nc.vector.tensor_scalar_mul(merged[:], partial[0], factor[:, 1:2])
-        for g in range(1, N_PIECES):
-            longer = held.tile([H, D], F32, name=f"merged{g}")
-            nc.vector.scalar_tensor_tensor(longer[:], partial[g], factor[:, g + 1 : g + 2], merged[:], op0=MULT, op1=ADD)
-            merged = longer
-        nc.sync.dma_start(out, merged[:])
+        late_factor = held.tile([H, 2], F32, name="late_factor")
+        nc.vector.tensor_scalar_mul(late_factor[:], rescale[:, N_PIECES - 1 : N_PIECES + 1], inv_den[:, 0:1])
+        merged1_over_den = held.tile([H, D], F32, name="merged1_over_den")
+        nc.vector.tensor_scalar_mul(merged1_over_den[:], merged1[:], inv_den[:, 0:1])
+        merged2_over_den = held.tile([H, D], F32, name="merged2_over_den")
+        nc.vector.scalar_tensor_tensor(
+            merged2_over_den[:], partial[LAST - 1][:], late_factor[:, 0:1], merged1_over_den[:], op0=MULT, op1=ADD
+        )
+        result = held.tile([H, D], F32, name="result")
+        nc.vector.scalar_tensor_tensor(
+            result[:], partial[LAST][:], late_factor[:, 1:2], merged2_over_den[:], op0=MULT, op1=ADD
+        )
+        nc.sync.dma_start(out, result[:])

@@ -15,6 +15,7 @@ N_PIECES = N // PIECE
 LAST = N_PIECES - 1
 BLOCK = 128
 LAST_PIECE_CHUNKS = (256, 128, 128)
+MULTIPLY_LAG = 3
 
 FLOPS = 2 * H * D * N + 2 * H * N * D
 
@@ -73,59 +74,65 @@ def tile_mm_kernel(tc, qt, k_pool, v, sinks, offs, out):
         nc.vector.memset(mass[:], 1.0)
         rescale = held.tile([H, N_PIECES + 1], F32, name="rescale")
 
-        flipped_banks = []
-        partial = []
-        for step in range(n_chunks + 1):
-            if step < n_chunks:
-                g, first, width = chunks[step]
-                blocks = width // BLOCK
-                weights = held.tile([H, width], BF16, name=f"weights{step}")
-                nc.scalar.activation(
-                    weights[:],
-                    scores[g][:, first : first + width],
-                    EXP,
-                    bias=neg_shift[:, g + 1 : g + 2],
-                    scale=SCALE,
-                    accum_out=mass[:, step + 1 : step + 2],
-                )
-                flipped_bank = banks.tile([BLOCK, width], BF16, name=f"flipped_bank{step}", tag="bank")
-                weights_by_block = weights[:].rearrange("h (p b) -> h b p", b=blocks)
-                for b in range(blocks):
-                    nc.tensor.transpose(
-                        flipped_bank[:, b * BLOCK : (b + 1) * BLOCK], weights_by_block[:, b, :], identity[:]
-                    )
-                flipped_banks.append(flipped_bank)
-                if g == LAST and first == 0:
-                    nc.scalar.activation(rescale[:], neg_shift[:], EXP, bias=neg_common[:, 0:1], scale=-1.0)
-            if step > 0:
-                c = step - 1
-                g, first, width = chunks[c]
-                blocks = width // BLOCK
-                flipped = held.tile([BLOCK, width], BF16, name=f"flipped{c}")
-                if g == LAST and first > 0:
-                    nc.scalar.copy(flipped[:], flipped_banks[c][:])
-                else:
-                    nc.vector.tensor_copy(flipped[:], flipped_banks[c][:])
-                if first == 0:
-                    partial.append(banks.tile([H, D], F32, name=f"partial{g}", tag="bank"))
-                for b in range(blocks):
-                    nc.tensor.matmul(
-                        partial[g][:],
-                        flipped[:, b * BLOCK : (b + 1) * BLOCK],
-                        values[c][:, b, :],
-                        start=(first == 0 and b == 0),
-                        stop=(first + width == PIECE and b == blocks - 1),
-                    )
+        flipped_banks = {}
+        flipped = {}
+        partial = {}
 
-        merged0 = held.tile([H, D], F32, name="merged0")
-        nc.vector.tensor_scalar_mul(merged0[:], partial[0][:], rescale[:, 1:2])
-        merged1 = held.tile([H, D], F32, name="merged1")
-        nc.vector.scalar_tensor_tensor(merged1[:], partial[1][:], rescale[:, 2:3], merged0[:], op0=MULT, op1=ADD)
+        def exp_and_flip(c):
+            g, first, width = chunks[c]
+            blocks = width // BLOCK
+            weights = held.tile([H, width], BF16, name=f"weights{c}")
+            nc.scalar.activation(
+                weights[:],
+                scores[g][:, first : first + width],
+                EXP,
+                bias=neg_shift[:, g + 1 : g + 2],
+                scale=SCALE,
+                accum_out=mass[:, c + 1 : c + 2],
+            )
+            flipped_banks[c] = banks.tile([BLOCK, width], BF16, name=f"flipped_bank{c}", tag="bank")
+            weights_by_block = weights[:].rearrange("h (p b) -> h b p", b=blocks)
+            for b in range(blocks):
+                nc.tensor.transpose(flipped_banks[c][:, b * BLOCK : (b + 1) * BLOCK], weights_by_block[:, b, :], identity[:])
+
+        def copy_out(c, engine_copy):
+            flipped[c] = held.tile([BLOCK, chunks[c][2]], BF16, name=f"flipped{c}")
+            engine_copy(flipped[c][:], flipped_banks[c][:])
+
+        def multiply(c):
+            g, first, width = chunks[c]
+            blocks = width // BLOCK
+            if first == 0:
+                partial[g] = banks.tile([H, D], F32, name=f"partial{g}", tag="bank")
+            for b in range(blocks):
+                nc.tensor.matmul(
+                    partial[g][:],
+                    flipped[c][:, b * BLOCK : (b + 1) * BLOCK],
+                    values[c][:, b, :],
+                    start=(first == 0 and b == 0),
+                    stop=(first + width == PIECE and b == blocks - 1),
+                )
+
         early_terms = held.tile([H, N_PIECES], F32, name="early_terms")
         early_den = held.tile([H, 1], F32, name="early_den")
-        nc.vector.scalar_tensor_tensor(
-            early_terms[:], mass[:, 0:N_PIECES], 1.0, rescale[:, 0:N_PIECES], op0=MULT, op1=MULT, accum_out=early_den[:]
-        )
+        for step in range(n_chunks):
+            exp_and_flip(step)
+            if step == LAST:
+                nc.scalar.activation(rescale[:], neg_shift[:], EXP, bias=neg_common[:, 0:1], scale=-1.0)
+                nc.vector.scalar_tensor_tensor(
+                    early_terms[:],
+                    mass[:, 0:N_PIECES],
+                    1.0,
+                    rescale[:, 0:N_PIECES],
+                    op0=MULT,
+                    op1=MULT,
+                    accum_out=early_den[:],
+                )
+            if 1 <= step <= LAST:
+                copy_out(step - 1, nc.vector.tensor_copy)
+            if step >= MULTIPLY_LAG:
+                multiply(step - MULTIPLY_LAG)
+
         last_terms = held.tile([H, n_chunks - LAST], F32, name="last_terms")
         den = held.tile([H, 1], F32, name="den")
         nc.vector.tensor_scalar(
@@ -137,12 +144,21 @@ def tile_mm_kernel(tc, qt, k_pool, v, sinks, offs, out):
             op1=ADD,
             accum_out=den[:],
         )
+        merged0 = held.tile([H, D], F32, name="merged0")
+        nc.vector.tensor_scalar_mul(merged0[:], partial[0][:], rescale[:, 1:2])
+        copy_out(LAST, nc.vector.tensor_copy)
+        for c in range(LAST + 1, n_chunks):
+            copy_out(c, nc.scalar.copy)
         inv_den = held.tile([H, 1], F32, name="inv_den")
         nc.vector.reciprocal(inv_den[:], den[:])
+        merged1 = held.tile([H, D], F32, name="merged1")
+        nc.vector.scalar_tensor_tensor(merged1[:], partial[1][:], rescale[:, 2:3], merged0[:], op0=MULT, op1=ADD)
         late_factor = held.tile([H, 2], F32, name="late_factor")
         nc.vector.tensor_scalar_mul(late_factor[:], rescale[:, N_PIECES - 1 : N_PIECES + 1], inv_den[:, 0:1])
         merged1_over_den = held.tile([H, D], F32, name="merged1_over_den")
         nc.vector.tensor_scalar_mul(merged1_over_den[:], merged1[:], inv_den[:, 0:1])
+        for c in range(n_chunks - MULTIPLY_LAG, n_chunks):
+            multiply(c)
         merged2_over_den = held.tile([H, D], F32, name="merged2_over_den")
         nc.vector.scalar_tensor_tensor(
             merged2_over_den[:], partial[LAST - 1][:], late_factor[:, 0:1], merged1_over_den[:], op0=MULT, op1=ADD

@@ -15,7 +15,7 @@ N_PIECES = N // PIECE
 LAST = N_PIECES - 1
 BLOCK = 128
 LAST_PIECE_CHUNKS = (256, 128, 128)
-MULTIPLY_LAG = 3
+MULTIPLY_LAG = 2
 
 FLOPS = 2 * H * D * N + 2 * H * N * D
 
@@ -72,7 +72,8 @@ def tile_mm_kernel(tc, qt, k_pool, v, sinks, offs, out):
 
         mass = held.tile([H, n_chunks + 1], F32, name="mass")
         nc.vector.memset(mass[:], 1.0)
-        rescale = held.tile([H, N_PIECES + 1], F32, name="rescale")
+        to_divide = held.tile([H, D + N_PIECES + 1], F32, name="to_divide")
+        rescale = to_divide[:, D : D + N_PIECES + 1]
 
         flipped_banks = {}
         flipped = {}
@@ -115,10 +116,12 @@ def tile_mm_kernel(tc, qt, k_pool, v, sinks, offs, out):
 
         early_terms = held.tile([H, N_PIECES], F32, name="early_terms")
         early_den = held.tile([H, 1], F32, name="early_den")
+        last_terms = held.tile([H, n_chunks - N_PIECES], F32, name="last_terms")
+        most_of_den = held.tile([H, 1], F32, name="most_of_den")
         for step in range(n_chunks):
             exp_and_flip(step)
             if step == LAST:
-                nc.scalar.activation(rescale[:], neg_shift[:], EXP, bias=neg_common[:, 0:1], scale=-1.0)
+                nc.scalar.activation(rescale, neg_shift[:], EXP, bias=neg_common[:, 0:1], scale=-1.0)
                 nc.vector.scalar_tensor_tensor(
                     early_terms[:],
                     mass[:, 0:N_PIECES],
@@ -130,41 +133,47 @@ def tile_mm_kernel(tc, qt, k_pool, v, sinks, offs, out):
                 )
             if 1 <= step <= LAST:
                 copy_out(step - 1, nc.vector.tensor_copy)
-            if step >= MULTIPLY_LAG:
+            if 0 <= step - MULTIPLY_LAG < LAST - 1:
                 multiply(step - MULTIPLY_LAG)
+            if step == n_chunks - 2:
+                nc.vector.tensor_scalar(
+                    last_terms[:],
+                    mass[:, N_PIECES:n_chunks],
+                    rescale[:, N_PIECES : N_PIECES + 1],
+                    early_den[:, 0:1],
+                    op0=MULT,
+                    op1=ADD,
+                    accum_out=most_of_den[:],
+                )
 
-        last_terms = held.tile([H, n_chunks - LAST], F32, name="last_terms")
         den = held.tile([H, 1], F32, name="den")
         nc.vector.tensor_scalar(
-            last_terms[:],
-            mass[:, N_PIECES : n_chunks + 1],
+            den[:],
+            mass[:, n_chunks : n_chunks + 1],
             rescale[:, N_PIECES : N_PIECES + 1],
-            early_den[:, 0:1],
+            most_of_den[:, 0:1],
             op0=MULT,
             op1=ADD,
-            accum_out=den[:],
         )
         merged0 = held.tile([H, D], F32, name="merged0")
         nc.vector.tensor_scalar_mul(merged0[:], partial[0][:], rescale[:, 1:2])
         copy_out(LAST, nc.vector.tensor_copy)
         for c in range(LAST + 1, n_chunks):
             copy_out(c, nc.scalar.copy)
+        multiply(LAST - 1)
         inv_den = held.tile([H, 1], F32, name="inv_den")
         nc.vector.reciprocal(inv_den[:], den[:])
         merged1 = held.tile([H, D], F32, name="merged1")
         nc.vector.scalar_tensor_tensor(merged1[:], partial[1][:], rescale[:, 2:3], merged0[:], op0=MULT, op1=ADD)
-        late_factor = held.tile([H, 2], F32, name="late_factor")
-        nc.vector.tensor_scalar_mul(late_factor[:], rescale[:, N_PIECES - 1 : N_PIECES + 1], inv_den[:, 0:1])
-        merged1_over_den = held.tile([H, D], F32, name="merged1_over_den")
-        nc.vector.tensor_scalar_mul(merged1_over_den[:], merged1[:], inv_den[:, 0:1])
-        for c in range(n_chunks - MULTIPLY_LAG, n_chunks):
+        nc.vector.scalar_tensor_tensor(to_divide[:, 0:D], partial[2][:], rescale[:, 3:4], merged1[:], op0=MULT, op1=ADD)
+        divided = held.tile([H, D + N_PIECES + 1], F32, name="divided")
+        nc.vector.tensor_scalar_mul(divided[:], to_divide[:], inv_den[:, 0:1])
+        merged_over_den = divided[:, 0:D]
+        factor = divided[:, D : D + N_PIECES + 1]
+        for c in range(LAST, n_chunks):
             multiply(c)
-        merged2_over_den = held.tile([H, D], F32, name="merged2_over_den")
-        nc.vector.scalar_tensor_tensor(
-            merged2_over_den[:], partial[LAST - 1][:], late_factor[:, 0:1], merged1_over_den[:], op0=MULT, op1=ADD
-        )
         result = held.tile([H, D], F32, name="result")
         nc.vector.scalar_tensor_tensor(
-            result[:], partial[LAST][:], late_factor[:, 1:2], merged2_over_den[:], op0=MULT, op1=ADD
+            result[:], partial[LAST][:], factor[:, LAST + 1 : LAST + 2], merged_over_den, op0=MULT, op1=ADD
         )
         nc.sync.dma_start(out, result[:])

@@ -14,7 +14,8 @@ PIECE = 512
 N_PIECES = N // PIECE
 LAST = N_PIECES - 1
 BLOCK = 128
-LAST_PIECE_CHUNKS = (256, 128, 128)
+PIECE_CHUNKS = ((512,), (512,), (256, 256), (256, 256))
+HALVES = 2
 MULTIPLY_LAG = 2
 
 FLOPS = 2 * H * D * N + 2 * H * N * D
@@ -25,10 +26,11 @@ def tile_mm_kernel(tc, qt, k_pool, v, sinks, offs, out):
     chunks = []
     for g in range(N_PIECES):
         first = 0
-        for width in LAST_PIECE_CHUNKS if g == LAST else (PIECE,):
-            chunks.append((g, first, width))
+        for i, width in enumerate(PIECE_CHUNKS[g]):
+            chunks.append((g, i, first, width))
             first += width
     n_chunks = len(chunks)
+    n_terms = HALVES * (N_PIECES + 1)
 
     with (
         tc.tile_pool(name="held", bufs=1) as held,
@@ -44,7 +46,7 @@ def tile_mm_kernel(tc, qt, k_pool, v, sinks, offs, out):
         sink = held.tile([H, 1], F32, name="sink")
         nc.scalar.dma_start(sink[:], sinks)
         values = []
-        for c, (g, first, width) in enumerate(chunks):
+        for c, (g, i, first, width) in enumerate(chunks):
             blocks = width // BLOCK
             chunk_values = held.tile([BLOCK, blocks, D], BF16, name=f"values{c}")
             chunk_rows = v[g * PIECE + first : g * PIECE + first + width, :]
@@ -70,17 +72,18 @@ def tile_mm_kernel(tc, qt, k_pool, v, sinks, offs, out):
         neg_common = held.tile([H, 1], F32, name="neg_common")
         nc.vector.tensor_reduce(neg_common[:], neg_shift[:], axis=ALONG_ROW, op=MIN)
 
-        mass = held.tile([H, n_chunks + 1], F32, name="mass")
-        nc.vector.memset(mass[:], 1.0)
-        to_divide = held.tile([H, D + N_PIECES + 1], F32, name="to_divide")
-        rescale = to_divide[:, D : D + N_PIECES + 1]
+        mass = held.tile([H, N_PIECES + 1, HALVES], F32, name="mass")
+        nc.vector.memset(mass[:], 0.0)
+        nc.vector.memset(mass[:, 0, 0:1], 1.0)
+        to_divide = held.tile([H, D + n_terms], F32, name="to_divide")
+        rescale = to_divide[:, D : D + n_terms].rearrange("h (t i) -> h t i", i=HALVES)
 
         flipped_banks = {}
         flipped = {}
         partial = {}
 
         def exp_and_flip(c):
-            g, first, width = chunks[c]
+            g, i, first, width = chunks[c]
             blocks = width // BLOCK
             weights = held.tile([H, width], BF16, name=f"weights{c}")
             nc.scalar.activation(
@@ -89,7 +92,7 @@ def tile_mm_kernel(tc, qt, k_pool, v, sinks, offs, out):
                 EXP,
                 bias=neg_shift[:, g + 1 : g + 2],
                 scale=SCALE,
-                accum_out=mass[:, c + 1 : c + 2],
+                accum_out=mass[:, g + 1, i : i + 1],
             )
             flipped_banks[c] = banks.tile([BLOCK, width], BF16, name=f"flipped_bank{c}", tag="bank")
             weights_by_block = weights[:].rearrange("h (p b) -> h b p", b=blocks)
@@ -97,11 +100,11 @@ def tile_mm_kernel(tc, qt, k_pool, v, sinks, offs, out):
                 nc.tensor.transpose(flipped_banks[c][:, b * BLOCK : (b + 1) * BLOCK], weights_by_block[:, b, :], identity[:])
 
         def copy_out(c, engine_copy):
-            flipped[c] = held.tile([BLOCK, chunks[c][2]], BF16, name=f"flipped{c}")
+            flipped[c] = held.tile([BLOCK, chunks[c][3]], BF16, name=f"flipped{c}")
             engine_copy(flipped[c][:], flipped_banks[c][:])
 
         def multiply(c):
-            g, first, width = chunks[c]
+            g, i, first, width = chunks[c]
             blocks = width // BLOCK
             if first == 0:
                 partial[g] = banks.tile([H, D], F32, name=f"partial{g}", tag="bank")
@@ -114,66 +117,57 @@ def tile_mm_kernel(tc, qt, k_pool, v, sinks, offs, out):
                     stop=(first + width == PIECE and b == blocks - 1),
                 )
 
-        early_terms = held.tile([H, N_PIECES], F32, name="early_terms")
-        early_den = held.tile([H, 1], F32, name="early_den")
-        last_terms = held.tile([H, n_chunks - N_PIECES], F32, name="last_terms")
-        most_of_den = held.tile([H, 1], F32, name="most_of_den")
         for step in range(n_chunks):
             exp_and_flip(step)
-            if step == LAST:
-                nc.scalar.activation(rescale, neg_shift[:], EXP, bias=neg_common[:, 0:1], scale=-1.0)
-                nc.vector.scalar_tensor_tensor(
-                    early_terms[:],
-                    mass[:, 0:N_PIECES],
-                    1.0,
-                    rescale[:, 0:N_PIECES],
-                    op0=MULT,
-                    op1=MULT,
-                    accum_out=early_den[:],
+            if chunks[step][0] == LAST and chunks[step][1] == 0:
+                nc.scalar.activation(
+                    rescale,
+                    neg_shift[:].unsqueeze(2).to_broadcast([H, N_PIECES + 1, HALVES]),
+                    EXP,
+                    bias=neg_common[:, 0:1],
+                    scale=-1.0,
                 )
-            if 1 <= step <= LAST:
+            if step >= 1:
                 copy_out(step - 1, nc.vector.tensor_copy)
-            if 0 <= step - MULTIPLY_LAG < LAST - 1:
+            if step >= MULTIPLY_LAG:
                 multiply(step - MULTIPLY_LAG)
-            if step == n_chunks - 2:
-                nc.vector.tensor_scalar(
-                    last_terms[:],
-                    mass[:, N_PIECES:n_chunks],
-                    rescale[:, N_PIECES : N_PIECES + 1],
-                    early_den[:, 0:1],
-                    op0=MULT,
-                    op1=ADD,
-                    accum_out=most_of_den[:],
-                )
 
+        mass_row = mass[:].rearrange("h t i -> h (t i)")
+        rescale_row = to_divide[:, D : D + n_terms]
+        most_terms = held.tile([H, n_terms - 1], F32, name="most_terms")
+        most_of_den = held.tile([H, 1], F32, name="most_of_den")
+        nc.vector.scalar_tensor_tensor(
+            most_terms[:],
+            mass_row[:, 0 : n_terms - 1],
+            1.0,
+            rescale_row[:, 0 : n_terms - 1],
+            op0=MULT,
+            op1=MULT,
+            accum_out=most_of_den[:],
+        )
         den = held.tile([H, 1], F32, name="den")
         nc.vector.tensor_scalar(
             den[:],
-            mass[:, n_chunks : n_chunks + 1],
-            rescale[:, N_PIECES : N_PIECES + 1],
+            mass_row[:, n_terms - 1 : n_terms],
+            rescale_row[:, n_terms - 1 : n_terms],
             most_of_den[:, 0:1],
             op0=MULT,
             op1=ADD,
         )
-        merged0 = held.tile([H, D], F32, name="merged0")
-        nc.vector.tensor_scalar_mul(merged0[:], partial[0][:], rescale[:, 1:2])
-        copy_out(LAST, nc.vector.tensor_copy)
-        for c in range(LAST + 1, n_chunks):
-            copy_out(c, nc.scalar.copy)
-        multiply(LAST - 1)
+        copy_out(n_chunks - 1, nc.scalar.copy)
         inv_den = held.tile([H, 1], F32, name="inv_den")
         nc.vector.reciprocal(inv_den[:], den[:])
+        merged0 = held.tile([H, D], F32, name="merged0")
+        nc.vector.tensor_scalar_mul(merged0[:], partial[0][:], rescale[:, 1, 0:1])
         merged1 = held.tile([H, D], F32, name="merged1")
-        nc.vector.scalar_tensor_tensor(merged1[:], partial[1][:], rescale[:, 2:3], merged0[:], op0=MULT, op1=ADD)
-        nc.vector.scalar_tensor_tensor(to_divide[:, 0:D], partial[2][:], rescale[:, 3:4], merged1[:], op0=MULT, op1=ADD)
-        divided = held.tile([H, D + N_PIECES + 1], F32, name="divided")
+        nc.vector.scalar_tensor_tensor(merged1[:], partial[1][:], rescale[:, 2, 0:1], merged0[:], op0=MULT, op1=ADD)
+        nc.vector.scalar_tensor_tensor(to_divide[:, 0:D], partial[2][:], rescale[:, 3, 0:1], merged1[:], op0=MULT, op1=ADD)
+        divided = held.tile([H, D + n_terms], F32, name="divided")
         nc.vector.tensor_scalar_mul(divided[:], to_divide[:], inv_den[:, 0:1])
-        merged_over_den = divided[:, 0:D]
-        factor = divided[:, D : D + N_PIECES + 1]
-        for c in range(LAST, n_chunks):
+        for c in range(n_chunks - MULTIPLY_LAG, n_chunks):
             multiply(c)
         result = held.tile([H, D], F32, name="result")
         nc.vector.scalar_tensor_tensor(
-            result[:], partial[LAST][:], factor[:, LAST + 1 : LAST + 2], merged_over_den, op0=MULT, op1=ADD
+            result[:], partial[LAST][:], divided[:, D + n_terms - 1 : D + n_terms], divided[:, 0:D], op0=MULT, op1=ADD
         )
         nc.sync.dma_start(out, result[:])

@@ -16,7 +16,8 @@ LAST = N_PIECES - 1
 BLOCK = 128
 PIECE_CHUNKS = ((512,), (512,), (256, 256), (256, 256))
 HALVES = 2
-MULTIPLY_LAG = 2
+FLIP_BANKS = ((0,), (1,), (6, 7), (0, 1))
+FIRST_SUM_BANK = 4
 
 FLOPS = 2 * H * D * N + 2 * H * N * D
 
@@ -29,13 +30,12 @@ def tile_mm_kernel(tc, qt, k_pool, v, sinks, offs, out):
         for i, width in enumerate(PIECE_CHUNKS[g]):
             chunks.append((g, i, first, width))
             first += width
-    n_chunks = len(chunks)
     n_terms = HALVES * (N_PIECES + 1)
 
     with (
         tc.tile_pool(name="held", bufs=1) as held,
         tc.tile_pool(name="ring", bufs=2) as ring,
-        tc.psum_pool(name="banks", bufs=8) as banks,
+        tc.psum_pool(name="banks", bufs=1) as banks,
     ):
         offsets = held.tile([128, N // 16], U16, name="offsets")
         nc.sync.dma_start(offsets[:], offs)
@@ -61,7 +61,7 @@ def tile_mm_kernel(tc, qt, k_pool, v, sinks, offs, out):
         neg_shift = held.tile([H, N_PIECES + 1], F32, name="neg_shift")
         nc.vector.tensor_scalar_mul(neg_shift[:, 0:1], sink[:], -1.0)
 
-        scores = [banks.tile([H, PIECE], F32, name=f"scores{g}", tag="bank") for g in range(N_PIECES)]
+        scores = [banks.tile([H, PIECE], F32, name=f"scores{g}", tag=f"bank{g}") for g in range(N_PIECES)]
         for g in range(N_PIECES):
             piece_offsets = offsets[:, g * (PIECE // 16) : (g + 1) * (PIECE // 16)]
             nc.tensor.matmul(scores[g][:], queries[:], keys[:].indirect(piece_offsets), start=True, stop=True)
@@ -70,13 +70,11 @@ def tile_mm_kernel(tc, qt, k_pool, v, sinks, offs, out):
                 neg_logits[:], scores[g][:], -SCALE, None, op0=MULT, op1=MIN, accum_out=neg_shift[:, g + 1 : g + 2]
             )
         neg_common = held.tile([H, 1], F32, name="neg_common")
-        nc.vector.tensor_reduce(neg_common[:], neg_shift[:], axis=ALONG_ROW, op=MIN)
 
         mass = held.tile([H, N_PIECES + 1, HALVES], F32, name="mass")
         nc.vector.memset(mass[:], 0.0)
         nc.vector.memset(mass[:, 0, 0:1], 1.0)
-        to_divide = held.tile([H, D + n_terms], F32, name="to_divide")
-        rescale = to_divide[:, D : D + n_terms].rearrange("h (t i) -> h t i", i=HALVES)
+        rescale = held.tile([H, N_PIECES + 1, HALVES], F32, name="rescale")
 
         flipped_banks = {}
         flipped = {}
@@ -94,7 +92,7 @@ def tile_mm_kernel(tc, qt, k_pool, v, sinks, offs, out):
                 scale=SCALE,
                 accum_out=mass[:, g + 1, i : i + 1],
             )
-            flipped_banks[c] = banks.tile([BLOCK, width], BF16, name=f"flipped_bank{c}", tag="bank")
+            flipped_banks[c] = banks.tile([BLOCK, width], BF16, name=f"flipped_bank{c}", tag=f"bank{FLIP_BANKS[g][i]}")
             weights_by_block = weights[:].rearrange("h (p b) -> h b p", b=blocks)
             for b in range(blocks):
                 nc.tensor.transpose(flipped_banks[c][:, b * BLOCK : (b + 1) * BLOCK], weights_by_block[:, b, :], identity[:])
@@ -107,7 +105,7 @@ def tile_mm_kernel(tc, qt, k_pool, v, sinks, offs, out):
             g, i, first, width = chunks[c]
             blocks = width // BLOCK
             if first == 0:
-                partial[g] = banks.tile([H, D], F32, name=f"partial{g}", tag="bank")
+                partial[g] = banks.tile([H, D], F32, name=f"partial{g}", tag=f"bank{FIRST_SUM_BANK + g}")
             for b in range(blocks):
                 nc.tensor.matmul(
                     partial[g][:],
@@ -117,57 +115,55 @@ def tile_mm_kernel(tc, qt, k_pool, v, sinks, offs, out):
                     stop=(first + width == PIECE and b == blocks - 1),
                 )
 
-        for step in range(n_chunks):
-            exp_and_flip(step)
-            if chunks[step][0] == LAST and chunks[step][1] == 0:
-                nc.scalar.activation(
-                    rescale,
-                    neg_shift[:].unsqueeze(2).to_broadcast([H, N_PIECES + 1, HALVES]),
-                    EXP,
-                    bias=neg_common[:, 0:1],
-                    scale=-1.0,
-                )
-            if step >= 1:
-                copy_out(step - 1, nc.vector.tensor_copy)
-            if step >= MULTIPLY_LAG:
-                multiply(step - MULTIPLY_LAG)
-
-        mass_row = mass[:].rearrange("h t i -> h (t i)")
-        rescale_row = to_divide[:, D : D + n_terms]
-        most_terms = held.tile([H, n_terms - 1], F32, name="most_terms")
-        most_of_den = held.tile([H, 1], F32, name="most_of_den")
-        nc.vector.scalar_tensor_tensor(
-            most_terms[:],
-            mass_row[:, 0 : n_terms - 1],
-            1.0,
-            rescale_row[:, 0 : n_terms - 1],
-            op0=MULT,
-            op1=MULT,
-            accum_out=most_of_den[:],
+        exp_and_flip(0)
+        exp_and_flip(1)
+        copy_out(0, nc.vector.tensor_copy)
+        nc.vector.tensor_reduce(neg_common[:], neg_shift[:], axis=ALONG_ROW, op=MIN)
+        exp_and_flip(2)
+        copy_out(1, nc.vector.tensor_copy)
+        exp_and_flip(3)
+        copy_out(2, nc.vector.tensor_copy)
+        multiply(0)
+        exp_and_flip(4)
+        nc.scalar.activation(
+            rescale[:],
+            neg_shift[:].unsqueeze(2).to_broadcast([H, N_PIECES + 1, HALVES]),
+            EXP,
+            bias=neg_common[:, 0:1],
+            scale=-1.0,
         )
-        den = held.tile([H, 1], F32, name="den")
-        nc.vector.tensor_scalar(
-            den[:],
-            mass_row[:, n_terms - 1 : n_terms],
-            rescale_row[:, n_terms - 1 : n_terms],
-            most_of_den[:, 0:1],
-            op0=MULT,
-            op1=ADD,
-        )
-        copy_out(n_chunks - 1, nc.scalar.copy)
-        inv_den = held.tile([H, 1], F32, name="inv_den")
-        nc.vector.reciprocal(inv_den[:], den[:])
+        copy_out(3, nc.vector.tensor_copy)
+        multiply(1)
         merged0 = held.tile([H, D], F32, name="merged0")
         nc.vector.tensor_scalar_mul(merged0[:], partial[0][:], rescale[:, 1, 0:1])
+        exp_and_flip(5)
+        terms = held.tile([H, n_terms], F32, name="terms")
+        den = held.tile([H, 1], F32, name="den")
+        nc.vector.scalar_tensor_tensor(
+            terms[:],
+            mass[:].rearrange("h t i -> h (t i)"),
+            1.0,
+            rescale[:].rearrange("h t i -> h (t i)"),
+            op0=MULT,
+            op1=MULT,
+            accum_out=den[:],
+        )
+        copy_out(4, nc.scalar.copy)
+        multiply(2)
+        inv_den = held.tile([H, 1], F32, name="inv_den")
+        nc.vector.reciprocal(inv_den[:], den[:])
         merged1 = held.tile([H, D], F32, name="merged1")
         nc.vector.scalar_tensor_tensor(merged1[:], partial[1][:], rescale[:, 2, 0:1], merged0[:], op0=MULT, op1=ADD)
-        nc.vector.scalar_tensor_tensor(to_divide[:, 0:D], partial[2][:], rescale[:, 3, 0:1], merged1[:], op0=MULT, op1=ADD)
-        divided = held.tile([H, D + n_terms], F32, name="divided")
-        nc.vector.tensor_scalar_mul(divided[:], to_divide[:], inv_den[:, 0:1])
-        for c in range(n_chunks - MULTIPLY_LAG, n_chunks):
-            multiply(c)
+        copy_out(5, nc.scalar.copy)
+        multiply(3)
+        divided2 = held.tile([H, D], F32, name="divided2")
+        nc.vector.tensor_scalar(divided2[:], partial[2][:], rescale[:, 3, 0:1], inv_den[:, 0:1], op0=MULT, op1=MULT)
+        last_factor = held.tile([H, 1], F32, name="last_factor")
+        nc.vector.tensor_scalar_mul(last_factor[:], rescale[:, LAST + 1, 0:1], inv_den[:, 0:1])
+        merged2 = held.tile([H, D], F32, name="merged2")
+        nc.vector.scalar_tensor_tensor(merged2[:], merged1[:], inv_den[:, 0:1], divided2[:], op0=MULT, op1=ADD)
+        multiply(4)
+        multiply(5)
         result = held.tile([H, D], F32, name="result")
-        nc.vector.scalar_tensor_tensor(
-            result[:], partial[LAST][:], divided[:, D + n_terms - 1 : D + n_terms], divided[:, 0:D], op0=MULT, op1=ADD
-        )
+        nc.vector.scalar_tensor_tensor(result[:], partial[LAST][:], last_factor[:, 0:1], merged2[:], op0=MULT, op1=ADD)
         nc.sync.dma_start(out, result[:])

@@ -95,7 +95,13 @@ def tile_mm_kernel(tc, qt, k_pool, v, sinks, offs, out):
             flipped_banks[c] = banks.tile([BLOCK, width], BF16, name=f"flipped_bank{c}", tag=f"bank{FLIP_BANKS[g][i]}")
             weights_by_block = weights[:].rearrange("h (p b) -> h b p", b=blocks)
             for b in range(blocks):
-                nc.tensor.transpose(flipped_banks[c][:, b * BLOCK : (b + 1) * BLOCK], weights_by_block[:, b, :], identity[:])
+                nc.tensor.matmul(
+                    flipped_banks[c][:, b * BLOCK : (b + 1) * BLOCK],
+                    weights_by_block[:, b, :],
+                    identity[:],
+                    start=True,
+                    stop=True,
+                )
 
         def copy_out(c, engine_copy):
             flipped[c] = held.tile([BLOCK, chunks[c][3]], BF16, name=f"flipped{c}")

@@ -6,7 +6,6 @@ from concourse.masks import make_identity
 BF16, F32, U16 = mybir.dt.bfloat16, mybir.dt.float32, mybir.dt.uint16
 EXP = mybir.ActivationFunctionType.Exp
 MULT, ADD, MIN = mybir.AluOpType.mult, mybir.AluOpType.add, mybir.AluOpType.min
-ALONG_ROW = mybir.AxisListType.X
 
 D, S, H, N = 128, 4096, 128, 2048
 SCALE = 1.0 / math.sqrt(D)
@@ -69,6 +68,7 @@ def tile_mm_kernel(tc, qt, k_pool, v, sinks, offs, out):
             nc.vector.tensor_scalar(
                 neg_logits[:], scores[g][:], -SCALE, None, op0=MULT, op1=MIN, accum_out=neg_shift[:, g + 1 : g + 2]
             )
+        neg_early = held.tile([H, 1], F32, name="neg_early")
         neg_common = held.tile([H, 1], F32, name="neg_common")
 
         mass = held.tile([H, N_PIECES + 1, HALVES], F32, name="mass")
@@ -124,7 +124,10 @@ def tile_mm_kernel(tc, qt, k_pool, v, sinks, offs, out):
         exp_and_flip(0)
         exp_and_flip(1)
         copy_out(0, nc.vector.tensor_copy)
-        nc.vector.tensor_reduce(neg_common[:], neg_shift[:], axis=ALONG_ROW, op=MIN)
+        nc.gpsimd.tensor_scalar(
+            neg_early[:], neg_shift[:, 1:2], neg_shift[:, 0:1], neg_shift[:, 2:3], op0=MIN, op1=MIN
+        )
+        nc.gpsimd.tensor_scalar(neg_common[:], neg_shift[:, 4:5], neg_shift[:, 3:4], neg_early[:, 0:1], op0=MIN, op1=MIN)
         exp_and_flip(2)
         copy_out(1, nc.vector.tensor_copy)
         exp_and_flip(3)

@@ -36,14 +36,14 @@ def tile_mm_kernel(tc, qt, k_pool, v, sinks, offs, out):
         tc.tile_pool(name="ring", bufs=2) as ring,
         tc.psum_pool(name="banks", bufs=1) as banks,
     ):
-        offsets = held.tile([128, N // 16], U16, name="offsets")
-        nc.sync.dma_start(offsets[:], offs)
         keys = held.tile([D, S], BF16, name="keys")
         nc.sync.dma_start(keys[:], k_pool)
+        offsets = held.tile([128, N // 16], U16, name="offsets")
+        nc.sync.dma_start(offsets[:], offs)
+        sink = held.tile([H, 1], F32, name="sink")
+        nc.sync.dma_start(sink[:], sinks)
         queries = held.tile([D, H], BF16, name="queries")
         nc.scalar.dma_start(queries[:], qt)
-        sink = held.tile([H, 1], F32, name="sink")
-        nc.scalar.dma_start(sink[:], sinks)
         values = []
         for c, (g, i, first, width) in enumerate(chunks):
             blocks = width // BLOCK

@@ -95,13 +95,11 @@ def tile_mm_kernel(tc, qt, k_pool, v, sinks, offs, out):
             flipped_banks[c] = banks.tile([BLOCK, width], BF16, name=f"flipped_bank{c}", tag=f"bank{FLIP_BANKS[g][i]}")
             weights_by_block = weights[:].rearrange("h (p b) -> h b p", b=blocks)
             for b in range(blocks):
-                nc.tensor.matmul(
-                    flipped_banks[c][:, b * BLOCK : (b + 1) * BLOCK],
-                    weights_by_block[:, b, :],
-                    identity[:],
-                    start=True,
-                    stop=True,
-                )
+                flip = flipped_banks[c][:, b * BLOCK : (b + 1) * BLOCK]
+                if g == 0:
+                    nc.tensor.matmul(flip, weights_by_block[:, b, :], identity[:], start=True, stop=True)
+                else:
+                    nc.tensor.transpose(flip, weights_by_block[:, b, :], identity[:])
 
         def copy_out(c, engine_copy):
             flipped[c] = held.tile([BLOCK, chunks[c][3]], BF16, name=f"flipped{c}")

@@ -13,6 +13,8 @@ PIECE = 512
 N_PIECES = N // PIECE
 LAST = N_PIECES - 1
 BLOCK = 128
+PAIR = 2
+N_PAIRS = N // (PAIR * BLOCK)
 PIECE_CHUNKS = ((512,), (512,), (256, 256), (256, 256))
 HALVES = 2
 FLIP_BANKS = ((0,), (1,), (6, 7), (0, 1))
@@ -37,22 +39,17 @@ def tile_mm_kernel(tc, qt, k_pool, v, sinks, offs, out):
         tc.psum_pool(name="banks", bufs=1) as banks,
     ):
         keys = held.tile([D, S], BF16, name="keys")
-        nc.sync.dma_start(keys[:], k_pool)
+        nc.scalar.dma_start(keys[:], k_pool)
         offsets = held.tile([128, N // 16], U16, name="offsets")
         nc.sync.dma_start(offsets[:], offs)
-        sink = held.tile([H, 1], F32, name="sink")
-        nc.sync.dma_start(sink[:], sinks)
         queries = held.tile([D, H], BF16, name="queries")
-        nc.scalar.dma_start(queries[:], qt)
-        values = []
-        for c, (g, i, first, width) in enumerate(chunks):
-            blocks = width // BLOCK
-            chunk_values = held.tile([BLOCK, blocks, D], BF16, name=f"values{c}")
-            chunk_rows = v[g * PIECE + first : g * PIECE + first + width, :]
-            nc.sync.dma_start(
-                chunk_values[:].rearrange("p b e -> p (b e)"), chunk_rows.rearrange("(p b) e -> p (b e)", b=blocks)
-            )
-            values.append(chunk_values)
+        nc.sync.dma_start(queries[:], qt)
+        sink = held.tile([H, 1], F32, name="sink")
+        nc.scalar.dma_start(sink[:], sinks)
+        values = held.tile([BLOCK, N_PAIRS, PAIR, D], BF16, name="values")
+        nc.scalar.dma_start(
+            values[:].rearrange("p k b e -> p k (b e)"), v.rearrange("(k p b) e -> p k (b e)", p=BLOCK, b=PAIR)
+        )
 
         identity = held.tile([H, H], BF16, name="identity")
         make_identity(nc, identity[:])
@@ -82,7 +79,6 @@ def tile_mm_kernel(tc, qt, k_pool, v, sinks, offs, out):
 
         def exp_and_flip(c):
             g, i, first, width = chunks[c]
-            blocks = width // BLOCK
             weights = held.tile([H, width], BF16, name=f"weights{c}")
             nc.scalar.activation(
                 weights[:],
@@ -93,13 +89,14 @@ def tile_mm_kernel(tc, qt, k_pool, v, sinks, offs, out):
                 accum_out=mass[:, g + 1, i : i + 1],
             )
             flipped_banks[c] = banks.tile([BLOCK, width], BF16, name=f"flipped_bank{c}", tag=f"bank{FLIP_BANKS[g][i]}")
-            weights_by_block = weights[:].rearrange("h (p b) -> h b p", b=blocks)
-            for b in range(blocks):
-                flip = flipped_banks[c][:, b * BLOCK : (b + 1) * BLOCK]
+            weights_by_block = weights[:].rearrange("h (k p b) -> h k b p", p=BLOCK, b=PAIR)
+            for n in range(width // BLOCK):
+                flip = flipped_banks[c][:, n * BLOCK : (n + 1) * BLOCK]
+                block = weights_by_block[:, n // PAIR, n % PAIR, :]
                 if g == 0:
-                    nc.tensor.matmul(flip, weights_by_block[:, b, :], identity[:], start=True, stop=True)
+                    nc.tensor.matmul(flip, block, identity[:], start=True, stop=True)
                 else:
-                    nc.tensor.transpose(flip, weights_by_block[:, b, :], identity[:])
+                    nc.tensor.transpose(flip, block, identity[:])
 
         def copy_out(c, engine_copy):
             flipped[c] = held.tile([BLOCK, chunks[c][3]], BF16, name=f"flipped{c}")
@@ -110,13 +107,14 @@ def tile_mm_kernel(tc, qt, k_pool, v, sinks, offs, out):
             blocks = width // BLOCK
             if first == 0:
                 partial[g] = banks.tile([H, D], F32, name=f"partial{g}", tag=f"bank{FIRST_SUM_BANK + g}")
-            for b in range(blocks):
+            first_pair = (g * PIECE + first) // (PAIR * BLOCK)
+            for n in range(blocks):
                 nc.tensor.matmul(
                     partial[g][:],
-                    flipped[c][:, b * BLOCK : (b + 1) * BLOCK],
-                    values[c][:, b, :],
-                    start=(first == 0 and b == 0),
-                    stop=(first + width == PIECE and b == blocks - 1),
+                    flipped[c][:, n * BLOCK : (n + 1) * BLOCK],
+                    values[:, first_pair + n // PAIR, n % PAIR, :],
+                    start=(first == 0 and n == 0),
+                    stop=(first + width == PIECE and n == blocks - 1),
                 )
 
         exp_and_flip(0)

@@ -12,12 +12,13 @@ SCALE = 1.0 / math.sqrt(D)
 PIECE = 512
 N_PIECES = N // PIECE
 LAST = N_PIECES - 1
+N_TERMS = N_PIECES + 1
 BLOCK = 128
 PAIR = 2
 N_PAIRS = N // (PAIR * BLOCK)
-PIECE_CHUNKS = ((512,), (512,), (256, 256), (256, 256))
+EXP_WIDTHS = (512, 512, 256, 512)
 HALVES = 2
-FLIP_BANKS = ((0,), (1,), (6, 7), (0, 1))
+CHUNKS = ((0, 0, 512, 0), (1, 0, 512, 1), (2, 0, 256, 6), (2, 256, 256, 7), (3, 0, 256, 0), (3, 256, 256, 1))
 FIRST_SUM_BANK = 4
 
 FLOPS = 2 * H * D * N + 2 * H * N * D
@@ -25,36 +26,28 @@ FLOPS = 2 * H * D * N + 2 * H * N * D
 
 def tile_mm_kernel(tc, qt, k_pool, v, sinks, offs, out):
     nc = tc.nc
-    chunks = []
-    for g in range(N_PIECES):
-        first = 0
-        for i, width in enumerate(PIECE_CHUNKS[g]):
-            chunks.append((g, i, first, width))
-            first += width
-    n_terms = HALVES * (N_PIECES + 1)
-
     with (
         tc.tile_pool(name="held", bufs=1) as held,
         tc.tile_pool(name="ring", bufs=2) as ring,
         tc.psum_pool(name="banks", bufs=1) as banks,
     ):
         keys = held.tile([D, S], BF16, name="keys")
-        nc.scalar.dma_start(keys[:], k_pool)
+        nc.sync.dma_start(keys[:], k_pool)
         offsets = held.tile([128, N // 16], U16, name="offsets")
         nc.sync.dma_start(offsets[:], offs)
-        queries = held.tile([D, H], BF16, name="queries")
-        nc.sync.dma_start(queries[:], qt)
         sink = held.tile([H, 1], F32, name="sink")
-        nc.scalar.dma_start(sink[:], sinks)
+        nc.sync.dma_start(sink[:], sinks)
+        queries = held.tile([D, H], BF16, name="queries")
+        nc.scalar.dma_start(queries[:], qt)
         values = held.tile([BLOCK, N_PAIRS, PAIR, D], BF16, name="values")
-        nc.scalar.dma_start(
+        nc.sync.dma_start(
             values[:].rearrange("p k b e -> p k (b e)"), v.rearrange("(k p b) e -> p k (b e)", p=BLOCK, b=PAIR)
         )
 
         identity = held.tile([H, H], BF16, name="identity")
         make_identity(nc, identity[:])
 
-        neg_shift = held.tile([H, N_PIECES + 1], F32, name="neg_shift")
+        neg_shift = held.tile([H, N_TERMS], F32, name="neg_shift")
         nc.vector.tensor_scalar_mul(neg_shift[:, 0:1], sink[:], -1.0)
 
         scores = [banks.tile([H, PIECE], F32, name=f"scores{g}", tag=f"bank{g}") for g in range(N_PIECES)]
@@ -65,84 +58,90 @@ def tile_mm_kernel(tc, qt, k_pool, v, sinks, offs, out):
             nc.vector.tensor_scalar(
                 neg_logits[:], scores[g][:], -SCALE, None, op0=MULT, op1=MIN, accum_out=neg_shift[:, g + 1 : g + 2]
             )
-        neg_early = held.tile([H, 1], F32, name="neg_early")
-        neg_common = held.tile([H, 1], F32, name="neg_common")
 
-        mass = held.tile([H, N_PIECES + 1, HALVES], F32, name="mass")
+        mass = held.tile([H, N_TERMS, HALVES], F32, name="mass")
         nc.vector.memset(mass[:], 0.0)
         nc.vector.memset(mass[:, 0, 0:1], 1.0)
-        rescale = held.tile([H, N_PIECES + 1, HALVES], F32, name="rescale")
 
+        weights = {}
         flipped_banks = {}
         flipped = {}
         partial = {}
 
-        def exp_and_flip(c):
-            g, i, first, width = chunks[c]
-            weights = held.tile([H, width], BF16, name=f"weights{c}")
-            nc.scalar.activation(
-                weights[:],
-                scores[g][:, first : first + width],
-                EXP,
-                bias=neg_shift[:, g + 1 : g + 2],
-                scale=SCALE,
-                accum_out=mass[:, g + 1, i : i + 1],
-            )
-            flipped_banks[c] = banks.tile([BLOCK, width], BF16, name=f"flipped_bank{c}", tag=f"bank{FLIP_BANKS[g][i]}")
-            weights_by_block = weights[:].rearrange("h (k p b) -> h k b p", p=BLOCK, b=PAIR)
+        def exp(g):
+            width = EXP_WIDTHS[g]
+            weights[g] = held.tile([H, PIECE], BF16, name=f"weights{g}")
+            for i in range(PIECE // width):
+                nc.scalar.activation(
+                    weights[g][:, i * width : (i + 1) * width],
+                    scores[g][:, i * width : (i + 1) * width],
+                    EXP,
+                    bias=neg_shift[:, g + 1 : g + 2],
+                    scale=SCALE,
+                    accum_out=mass[:, g + 1, i : i + 1],
+                )
+
+        def flip(c):
+            g, first, width, bank = CHUNKS[c]
+            flipped_banks[c] = banks.tile([BLOCK, width], BF16, name=f"flipped_bank{c}", tag=f"bank{bank}")
+            by_block = weights[g][:, first : first + width].rearrange("h (k p b) -> h k b p", p=BLOCK, b=PAIR)
             for n in range(width // BLOCK):
-                flip = flipped_banks[c][:, n * BLOCK : (n + 1) * BLOCK]
-                block = weights_by_block[:, n // PAIR, n % PAIR, :]
+                flip_out = flipped_banks[c][:, n * BLOCK : (n + 1) * BLOCK]
+                block = by_block[:, n // PAIR, n % PAIR, :]
                 if g == 0:
-                    nc.tensor.matmul(flip, block, identity[:], start=True, stop=True)
+                    nc.tensor.matmul(flip_out, block, identity[:], start=True, stop=True)
                 else:
-                    nc.tensor.transpose(flip, block, identity[:])
+                    nc.tensor.transpose(flip_out, block, identity[:])
 
         def copy_out(c, engine_copy):
-            flipped[c] = held.tile([BLOCK, chunks[c][3]], BF16, name=f"flipped{c}")
+            flipped[c] = held.tile([BLOCK, CHUNKS[c][2]], BF16, name=f"flipped{c}")
             engine_copy(flipped[c][:], flipped_banks[c][:])
 
         def multiply(c):
-            g, i, first, width = chunks[c]
-            blocks = width // BLOCK
+            g, first, width, bank = CHUNKS[c]
             if first == 0:
                 partial[g] = banks.tile([H, D], F32, name=f"partial{g}", tag=f"bank{FIRST_SUM_BANK + g}")
             first_pair = (g * PIECE + first) // (PAIR * BLOCK)
-            for n in range(blocks):
+            for n in range(width // BLOCK):
                 nc.tensor.matmul(
                     partial[g][:],
                     flipped[c][:, n * BLOCK : (n + 1) * BLOCK],
                     values[:, first_pair + n // PAIR, n % PAIR, :],
                     start=(first == 0 and n == 0),
-                    stop=(first + width == PIECE and n == blocks - 1),
+                    stop=(first + width == PIECE and n == width // BLOCK - 1),
                 )
 
-        exp_and_flip(0)
-        exp_and_flip(1)
+        exp(0)
+        flip(0)
+        exp(1)
+        flip(1)
         copy_out(0, nc.vector.tensor_copy)
+        neg_early = held.tile([H, 1], F32, name="neg_early")
         nc.gpsimd.tensor_scalar(
             neg_early[:], neg_shift[:, 1:2], neg_shift[:, 0:1], neg_shift[:, 2:3], op0=MIN, op1=MIN
         )
+        neg_common = held.tile([H, 1], F32, name="neg_common")
         nc.gpsimd.tensor_scalar(neg_common[:], neg_shift[:, 4:5], neg_shift[:, 3:4], neg_early[:, 0:1], op0=MIN, op1=MIN)
-        exp_and_flip(2)
+        exp(2)
         copy_out(1, nc.vector.tensor_copy)
-        exp_and_flip(3)
+        flip(2)
+        flip(3)
         copy_out(2, nc.vector.tensor_copy)
         multiply(0)
-        exp_and_flip(4)
+        exp(3)
+        rescale = held.tile([H, N_TERMS, HALVES], F32, name="rescale")
         nc.scalar.activation(
             rescale[:],
-            neg_shift[:].unsqueeze(2).to_broadcast([H, N_PIECES + 1, HALVES]),
+            neg_shift[:].unsqueeze(2).to_broadcast([H, N_TERMS, HALVES]),
             EXP,
             bias=neg_common[:, 0:1],
             scale=-1.0,
         )
         copy_out(3, nc.vector.tensor_copy)
         multiply(1)
-        merged0 = held.tile([H, D], F32, name="merged0")
-        nc.vector.tensor_scalar_mul(merged0[:], partial[0][:], rescale[:, 1, 0:1])
-        exp_and_flip(5)
-        terms = held.tile([H, n_terms], F32, name="terms")
+        flip(4)
+        flip(5)
+        terms = held.tile([H, N_TERMS * HALVES], F32, name="terms")
         den = held.tile([H, 1], F32, name="den")
         nc.vector.scalar_tensor_tensor(
             terms[:],
@@ -153,7 +152,9 @@ def tile_mm_kernel(tc, qt, k_pool, v, sinks, offs, out):
             op1=MULT,
             accum_out=den[:],
         )
-        copy_out(4, nc.scalar.copy)
+        merged0 = held.tile([H, D], F32, name="merged0")
+        nc.vector.tensor_scalar_mul(merged0[:], partial[0][:], rescale[:, 1, 0:1])
+        copy_out(4, nc.vector.tensor_copy)
         multiply(2)
         inv_den = held.tile([H, 1], F32, name="inv_den")
         nc.vector.reciprocal(inv_den[:], den[:])

import math

import concourse.mybir as mybir
from concourse.masks import make_identity

BF16, F32, U16 = mybir.dt.bfloat16, mybir.dt.float32, mybir.dt.uint16
EXP = mybir.ActivationFunctionType.Exp
MULT, ADD, MIN = mybir.AluOpType.mult, mybir.AluOpType.add, mybir.AluOpType.min

D, S, H, N = 128, 4096, 128, 2048
SCALE = 1.0 / math.sqrt(D)
PIECE = 512
N_PIECES = N // PIECE
LAST = N_PIECES - 1
N_TERMS = N_PIECES + 1
BLOCK = 128
PAIR = 2
N_PAIRS = N // (PAIR * BLOCK)
EXP_WIDTHS = (512, 512, 256, 512)
HALVES = 2
CHUNKS = ((0, 0, 512, 0), (1, 0, 512, 1), (2, 0, 256, 6), (2, 256, 256, 7), (3, 0, 256, 0), (3, 256, 256, 1))
FIRST_SUM_BANK = 4

FLOPS = 2 * H * D * N + 2 * H * N * D


def tile_mm_kernel(tc, qt, k_pool, v, sinks, offs, out):
    nc = tc.nc
    with (
        tc.tile_pool(name="held", bufs=1) as held,
        tc.tile_pool(name="ring", bufs=2) as ring,
        tc.psum_pool(name="banks", bufs=1) as banks,
    ):
        keys = held.tile([D, S], BF16, name="keys")
        nc.sync.dma_start(keys[:], k_pool)
        offsets = held.tile([128, N // 16], U16, name="offsets")
        nc.sync.dma_start(offsets[:], offs)
        sink = held.tile([H, 1], F32, name="sink")
        nc.sync.dma_start(sink[:], sinks)
        queries = held.tile([D, H], BF16, name="queries")
        nc.scalar.dma_start(queries[:], qt)
        values = held.tile([BLOCK, N_PAIRS, PAIR, D], BF16, name="values")
        nc.sync.dma_start(
            values[:].rearrange("p k b e -> p k (b e)"), v.rearrange("(k p b) e -> p k (b e)", p=BLOCK, b=PAIR)
        )

        identity = held.tile([H, H], BF16, name="identity")
        make_identity(nc, identity[:])

        neg_shift = held.tile([H, N_TERMS], F32, name="neg_shift")
        nc.vector.tensor_scalar_mul(neg_shift[:, 0:1], sink[:], -1.0)

        scores = [banks.tile([H, PIECE], F32, name=f"scores{g}", tag=f"bank{g}") for g in range(N_PIECES)]
        for g in range(N_PIECES):
            piece_offsets = offsets[:, g * (PIECE // 16) : (g + 1) * (PIECE // 16)]
            nc.tensor.matmul(scores[g][:], queries[:], keys[:].indirect(piece_offsets), start=True, stop=True)
            neg_logits = ring.tile([H, PIECE], F32, name="neg_logits")
            nc.vector.tensor_scalar(
                neg_logits[:], scores[g][:], -SCALE, None, op0=MULT, op1=MIN, accum_out=neg_shift[:, g + 1 : g + 2]
            )

        mass = held.tile([H, N_TERMS, HALVES], F32, name="mass")
        nc.vector.memset(mass[:], 0.0)
        nc.vector.memset(mass[:, 0, 0:1], 1.0)

        weights = {}
        flipped_banks = {}
        flipped = {}
        partial = {}

        def exp(g):
            width = EXP_WIDTHS[g]
            weights[g] = held.tile([H, PIECE], BF16, name=f"weights{g}")
            for i in range(PIECE // width):
                nc.scalar.activation(
                    weights[g][:, i * width : (i + 1) * width],
                    scores[g][:, i * width : (i + 1) * width],
                    EXP,
                    bias=neg_shift[:, g + 1 : g + 2],
                    scale=SCALE,
                    accum_out=mass[:, g + 1, i : i + 1],
                )

        def flip(c):
            g, first, width, bank = CHUNKS[c]
            flipped_banks[c] = banks.tile([BLOCK, width], BF16, name=f"flipped_bank{c}", tag=f"bank{bank}")
            by_block = weights[g][:, first : first + width].rearrange("h (k p b) -> h k b p", p=BLOCK, b=PAIR)
            for n in range(width // BLOCK):
                flip_out = flipped_banks[c][:, n * BLOCK : (n + 1) * BLOCK]
                block = by_block[:, n // PAIR, n % PAIR, :]
                if g == 0:
                    nc.tensor.matmul(flip_out, block, identity[:], start=True, stop=True)
                else:
                    nc.tensor.transpose(flip_out, block, identity[:])

        def copy_out(c, engine_copy):
            flipped[c] = held.tile([BLOCK, CHUNKS[c][2]], BF16, name=f"flipped{c}")
            engine_copy(flipped[c][:], flipped_banks[c][:])

        def multiply(c):
            g, first, width, bank = CHUNKS[c]
            if first == 0:
                partial[g] = banks.tile([H, D], F32, name=f"partial{g}", tag=f"bank{FIRST_SUM_BANK + g}")
            first_pair = (g * PIECE + first) // (PAIR * BLOCK)
            for n in range(width // BLOCK):
                nc.tensor.matmul(
                    partial[g][:],
                    flipped[c][:, n * BLOCK : (n + 1) * BLOCK],
                    values[:, first_pair + n // PAIR, n % PAIR, :],
                    start=(first == 0 and n == 0),
                    stop=(first + width == PIECE and n == width // BLOCK - 1),
                )

        exp(0)
        flip(0)
        exp(1)
        flip(1)
        copy_out(0, nc.vector.tensor_copy)
        neg_early = held.tile([H, 1], F32, name="neg_early")
        nc.gpsimd.tensor_scalar(
            neg_early[:], neg_shift[:, 1:2], neg_shift[:, 0:1], neg_shift[:, 2:3], op0=MIN, op1=MIN
        )
        neg_common = held.tile([H, 1], F32, name="neg_common")
        nc.gpsimd.tensor_scalar(neg_common[:], neg_shift[:, 4:5], neg_shift[:, 3:4], neg_early[:, 0:1], op0=MIN, op1=MIN)
        exp(2)
        copy_out(1, nc.vector.tensor_copy)
        flip(2)
        flip(3)
        copy_out(2, nc.vector.tensor_copy)
        multiply(0)
        exp(3)
        rescale = held.tile([H, N_TERMS, HALVES], F32, name="rescale")
        nc.scalar.activation(
            rescale[:],
            neg_shift[:].unsqueeze(2).to_broadcast([H, N_TERMS, HALVES]),
            EXP,
            bias=neg_common[:, 0:1],
            scale=-1.0,
        )
        copy_out(3, nc.vector.tensor_copy)
        multiply(1)
        flip(4)
        flip(5)
        terms = held.tile([H, N_TERMS * HALVES], F32, name="terms")
        den = held.tile([H, 1], F32, name="den")
        nc.vector.scalar_tensor_tensor(
            terms[:],
            mass[:].rearrange("h t i -> h (t i)"),
            1.0,
            rescale[:].rearrange("h t i -> h (t i)"),
            op0=MULT,
            op1=MULT,
            accum_out=den[:],
        )
        merged0 = held.tile([H, D], F32, name="merged0")
        nc.vector.tensor_scalar_mul(merged0[:], partial[0][:], rescale[:, 1, 0:1])
        copy_out(4, nc.vector.tensor_copy)
        multiply(2)
        inv_den = held.tile([H, 1], F32, name="inv_den")
        nc.vector.reciprocal(inv_den[:], den[:])
        merged1 = held.tile([H, D], F32, name="merged1")
        nc.vector.scalar_tensor_tensor(merged1[:], partial[1][:], rescale[:, 2, 0:1], merged0[:], op0=MULT, op1=ADD)
        copy_out(5, nc.scalar.copy)
        multiply(3)
        divided2 = held.tile([H, D], F32, name="divided2")
        nc.vector.tensor_scalar(divided2[:], partial[2][:], rescale[:, 3, 0:1], inv_den[:, 0:1], op0=MULT, op1=MULT)
        last_factor = held.tile([H, 1], F32, name="last_factor")
        nc.vector.tensor_scalar_mul(last_factor[:], rescale[:, LAST + 1, 0:1], inv_den[:, 0:1])
        merged2 = held.tile([H, D], F32, name="merged2")
        nc.vector.scalar_tensor_tensor(merged2[:], merged1[:], inv_den[:, 0:1], divided2[:], op0=MULT, op1=ADD)
        multiply(4)
        multiply(5)
        result = held.tile([H, D], F32, name="result")
        nc.vector.scalar_tensor_tensor(result[:], partial[LAST][:], last_factor[:, 0:1], merged2[:], op0=MULT, op1=ADD)
        nc.sync.dma_start(out, result[:])
